import numpy as np
import ml_dtypes

BF16 = ml_dtypes.bfloat16


def bf(x):
    return np.asarray(x, np.float32).astype(BF16)


def f32(x):
    return np.asarray(x, np.float32)


def f64(x):
    return np.asarray(x).astype(np.float64)


def striped(idx):
    return np.tile(idx.reshape(-1, 16).T, (8, 1))


B, CIN, H, W, KH, KW, PAD, O, DEPTH, LEAVES, NODES, GATES, C, S, N = 2, 64, 16, 16, 3, 3, 1, 128, 3, 8, 7, 16, 512, 576, 1024

COEFF = np.array([
    [0., 0., 0., 0.],
    [0., 0., 0., 1.],
    [0., 1., 0., -1.],
    [0., 1., 0., 0.],
    [0., 0., 1., -1.],
    [0., 0., 1., 0.],
    [0., 1., 1., -2.],
    [0., 1., 1., -1.],
    [1., -1., -1., 1.],
    [1., -1., -1., 2.],
    [1., 0., -1., 0.],
    [1., 0., -1., 1.],
    [1., -1., 0., 0.],
    [1., -1., 0., 1.],
    [1., 0., 0., -1.],
    [1., 0., 0., 0.],
], np.float64)


def unfold(img):
    xp = np.pad(img, ((0, 0), (0, 0), (PAD, PAD), (PAD, PAD)))
    cols = np.stack([xp[:, :, r:r + H, s:s + W] for r in range(KH) for s in range(KW)], axis=2)
    return cols.reshape(B, S, H * W).transpose(0, 2, 1).reshape(C, S)


def gate_weights(logits):
    e = np.exp(f64(logits))
    p = e / e.sum(axis=0, keepdims=True)
    return [(COEFF[:, t:t + 1] * p).sum(axis=0) for t in range(COEFF.shape[1])]


def setup_inputs():
    img = np.random.random_sample((B, CIN, H, W))
    return {"x": f32(unfold(img)), "logits": f32(3.0 * np.random.standard_normal((GATES, NODES * O))), "offs": striped(np.random.permutation(np.tile(np.arange(S), 2))[:N])}


def reference(x, logits, offs):
    idx = offs[:16].T.reshape(-1)
    w0, w1, w2, w3 = gate_weights(logits)
    cur = f64(x)[:, idx]
    lo = 0
    for _ in range(DEPTH):
        half = cur.shape[1] // 2
        a, b = cur[:, :half], cur[:, half:]
        sl = slice(lo, lo + half)
        cur = a * (w1[sl] + w3[sl] * b) + (w0[sl] + w2[sl] * b)
        lo += half
    return cur

@@ -1,0 +1,127 @@
+import concourse.mybir as mybir
+from concourse.masks import make_identity
+
+F32 = mybir.dt.float32
+U16 = mybir.dt.uint16
+ALU = mybir.AluOpType
+ACT = mybir.ActivationFunctionType
+AXIS = mybir.AxisListType
+
+P = 128
+ROWS, COLS = 512, 576
+ROW_BLOCKS = ROWS // P
+LIST = 1024
+KINDS = 16
+GATES = 896
+GATE_BLOCKS = GATES // P
+LEVEL_GATES = (512, 256, 128)
+BANK = 512
+
+
+def tile_logictreeconv2d_kernel(tc, x, logits, offs, out):
+    nc = tc.nc
+    with (
+        tc.tile_pool(name="held", bufs=1) as held,
+        tc.tile_pool(name="work", bufs=2) as work,
+        tc.psum_pool(name="psum", bufs=2) as psum,
+    ):
+        offsets = held.tile([P, LIST // 16], U16, name="offsets")
+        nc.sync.dma_start(offsets[:], offs)
+
+        kind_rows = held.tile([KINDS * GATE_BLOCKS, P], F32, name="kind_rows")
+        nc.scalar.dma_start(kind_rows[:], logits.rearrange("k (g n) -> (k g) n", n=P))
+
+        windows = []
+        for r in range(ROW_BLOCKS):
+            window = held.tile([P, COLS], F32, name=f"window{r}")
+            queue = nc.sync if r % 2 == 0 else nc.scalar
+            queue.dma_start(window[:], x[r * P : (r + 1) * P, :])
+            windows.append(window)
+
+        identity = held.tile([P, P], F32, name="identity")
+        make_identity(nc, identity[:])
+
+        flipped = psum.tile([P, KINDS * GATE_BLOCKS], F32, name="flipped")
+        nc.tensor.transpose(
+            flipped[:], kind_rows[:], identity[: KINDS * GATE_BLOCKS, : KINDS * GATE_BLOCKS]
+        )
+        by_kind = flipped[:].rearrange("p (k g) -> p k g", g=GATE_BLOCKS)
+
+        top = held.tile([P, GATE_BLOCKS], F32, name="top")
+        nc.vector.reduce_max(top[:], by_kind.rearrange("p k g -> p g k"), axis=AXIS.X)
+        expo = held.tile([P, KINDS, GATE_BLOCKS], F32, name="expo")
+        nc.vector.tensor_sub(
+            expo[:], by_kind, top[:].unsqueeze(1).to_broadcast([P, KINDS, GATE_BLOCKS])
+        )
+        nc.scalar.activation(expo[:], expo[:], ACT.Exp)
+        total = held.tile([P, GATE_BLOCKS], F32, name="total")
+        nc.vector.reduce_sum(total[:], expo[:].rearrange("p k g -> p g k"), axis=AXIS.X)
+
+        corner = held.tile([P, 4, GATE_BLOCKS], F32, name="corner")
+        for t in range(4):
+            with_bit = expo[:].rearrange("p (hi two lo) g -> p two g hi lo", two=2, lo=2**t)
+            nc.vector.reduce_sum(corner[:, t, :], with_bit[:, 1], axis=AXIS.XY)
+        nc.vector.reciprocal(total[:], total[:])
+        nc.vector.tensor_mul(
+            corner[:], corner[:], total[:].unsqueeze(1).to_broadcast([P, 4, GATE_BLOCKS])
+        )
+
+        weight = held.tile([P, 4, GATE_BLOCKS], F32, name="weight")
+        nc.vector.tensor_copy(weight[:, 0, :], corner[:, 3, :])
+        nc.vector.tensor_sub(
+            weight[:, 1:3, :],
+            corner[:, 1:3, :],
+            corner[:, 3:4, :].to_broadcast([P, 2, GATE_BLOCKS]),
+        )
+        nc.vector.tensor_sub(weight[:, 3, :], corner[:, 0, :], corner[:, 1, :])
+        nc.vector.tensor_sub(weight[:, 3, :], weight[:, 3, :], weight[:, 2, :])
+
+        rows = []
+        for t in range(4):
+            row = held.tile([P, GATES], F32, name=f"row{t}")
+            for lo in range(0, GATES, BANK):
+                width = min(BANK, GATES - lo)
+                spread = psum.tile([P, BANK], F32, name="spread")
+                for g in range(width // P):
+                    column = weight[:, t, lo // P + g : lo // P + g + 1]
+                    nc.tensor.transpose(
+                        spread[:, g * P : (g + 1) * P], column.to_broadcast([P, P]), identity[:]
+                    )
+                nc.scalar.copy(row[:, lo : lo + width], spread[:, :width])
+            rows.append(row)
+        w0, w1, w2, w3 = rows
+
+        half = LIST // 2
+        for r in range(ROW_BLOCKS):
+            n = LEVEL_GATES[0]
+            bracket = work.tile([P, n], F32, name="bracket")
+            nc.vector.tensor_tensor(
+                bracket[:], windows[r][:].indirect(offsets[:, half // 16 :]), w3[:, :n], ALU.mult
+            )
+            nc.vector.tensor_add(bracket[:], bracket[:], w1[:, :n])
+            rest = work.tile([P, n], F32, name="rest")
+            nc.vector.tensor_tensor(
+                rest[:], windows[r][:].indirect(offsets[:, half // 16 :]), w2[:, :n], ALU.mult
+            )
+            nc.vector.tensor_add(rest[:], rest[:], w0[:, :n])
+            level = work.tile([P, n], F32, name="level")
+            nc.vector.tensor_tensor(
+                level[:], windows[r][:].indirect(offsets[:, : half // 16]), bracket[:], ALU.mult
+            )
+            nc.vector.tensor_add(level[:], level[:], rest[:])
+
+            lo = n
+            for n in LEVEL_GATES[1:]:
+                a, b = level[:, :n], level[:, n : 2 * n]
+                bracket = work.tile([P, n], F32, name="bracket")
+                nc.vector.tensor_mul(bracket[:], b, w3[:, lo : lo + n])
+                nc.vector.tensor_add(bracket[:], bracket[:], w1[:, lo : lo + n])
+                rest = work.tile([P, n], F32, name="rest")
+                nc.vector.tensor_mul(rest[:], b, w2[:, lo : lo + n])
+                nc.vector.tensor_add(rest[:], rest[:], w0[:, lo : lo + n])
+                level = work.tile([P, n], F32, name="level")
+                nc.vector.tensor_mul(level[:], a, bracket[:])
+                nc.vector.tensor_add(level[:], level[:], rest[:])
+                lo += n
+
+            nc.sync.dma_start(out[r * P : (r + 1) * P, :], level[:])

@@ -11,18 +11,16 @@ P = 128
 ROWS, COLS = 512, 576
 ROW_BLOCKS = ROWS // P
 LIST = 1024
+HALF = LIST // 2
 KINDS = 16
-GATES = 896
-GATE_BLOCKS = GATES // P
-LEVEL_GATES = (512, 256, 128)
-BANK = 512
+GATE_BLOCKS = 7
 
 
 def tile_logictreeconv2d_kernel(tc, x, logits, offs, out):
     nc = tc.nc
     with (
         tc.tile_pool(name="held", bufs=1) as held,
-        tc.tile_pool(name="work", bufs=2) as work,
+        tc.tile_pool(name="work", bufs=3) as work,
         tc.psum_pool(name="psum", bufs=2) as psum,
     ):
         offsets = held.tile([P, LIST // 16], U16, name="offsets")
@@ -41,7 +39,12 @@ def tile_logictreeconv2d_kernel(tc, x, logits, offs, out):
         identity = held.tile([P, P], F32, name="identity")
         make_identity(nc, identity[:])
 
-        flipped = psum.tile([P, KINDS * GATE_BLOCKS], F32, name="flipped")
+        def add_flipped(acc, term, start, stop):
+            nc.tensor.matmul(
+                acc, lhsT=term, rhs=identity[:], is_transpose=True, start=start, stop=stop
+            )
+
+        flipped = psum.tile([P, KINDS * GATE_BLOCKS], F32, name="flipped", bufs=1)
         nc.tensor.transpose(
             flipped[:], kind_rows[:], identity[: KINDS * GATE_BLOCKS, : KINDS * GATE_BLOCKS]
         )
@@ -57,71 +60,85 @@ def tile_logictreeconv2d_kernel(tc, x, logits, offs, out):
         total = held.tile([P, GATE_BLOCKS], F32, name="total")
         nc.vector.reduce_sum(total[:], expo[:].rearrange("p k g -> p g k"), axis=AXIS.X)
 
-        corner = held.tile([P, 4, GATE_BLOCKS], F32, name="corner")
-        for t in range(4):
-            with_bit = expo[:].rearrange("p (hi two lo) g -> p two g hi lo", two=2, lo=2**t)
-            nc.vector.reduce_sum(corner[:, t, :], with_bit[:, 1], axis=AXIS.XY)
+        weight = held.tile([P, 4, GATE_BLOCKS], F32, name="weight")
+        for t, bit in enumerate((3, 1, 2, 0)):
+            with_bit = expo[:].rearrange("p (hi two lo) g -> p two g hi lo", two=2, lo=2**bit)
+            nc.vector.reduce_sum(weight[:, t, :], with_bit[:, 1], axis=AXIS.XY)
         nc.vector.reciprocal(total[:], total[:])
         nc.vector.tensor_mul(
-            corner[:], corner[:], total[:].unsqueeze(1).to_broadcast([P, 4, GATE_BLOCKS])
+            weight[:], weight[:], total[:].unsqueeze(1).to_broadcast([P, 4, GATE_BLOCKS])
         )
-
-        weight = held.tile([P, 4, GATE_BLOCKS], F32, name="weight")
-        nc.vector.tensor_copy(weight[:, 0, :], corner[:, 3, :])
+        nc.vector.tensor_sub(weight[:, 3, :], weight[:, 3, :], weight[:, 1, :])
         nc.vector.tensor_sub(
             weight[:, 1:3, :],
-            corner[:, 1:3, :],
-            corner[:, 3:4, :].to_broadcast([P, 2, GATE_BLOCKS]),
+            weight[:, 1:3, :],
+            weight[:, 0:1, :].to_broadcast([P, 2, GATE_BLOCKS]),
         )
-        nc.vector.tensor_sub(weight[:, 3, :], corner[:, 0, :], corner[:, 1, :])
         nc.vector.tensor_sub(weight[:, 3, :], weight[:, 3, :], weight[:, 2, :])
 
-        rows = []
-        for t in range(4):
-            row = held.tile([P, GATES], F32, name=f"row{t}")
-            for lo in range(0, GATES, BANK):
-                width = min(BANK, GATES - lo)
-                spread = psum.tile([P, BANK], F32, name="spread")
-                for g in range(width // P):
-                    column = weight[:, t, lo // P + g : lo // P + g + 1]
-                    nc.tensor.transpose(
-                        spread[:, g * P : (g + 1) * P], column.to_broadcast([P, P]), identity[:]
-                    )
-                nc.scalar.copy(row[:, lo : lo + width], spread[:, :width])
-            rows.append(row)
-        w0, w1, w2, w3 = rows
+        row = {}
+        for t in (2, 3, 1, 0):
+            spread = psum.tile([P, HALF], F32, name="spread")
+            for g in range(HALF // P):
+                nc.tensor.transpose(
+                    spread[:, g * P : (g + 1) * P],
+                    weight[:, t, g : g + 1].to_broadcast([P, P]),
+                    identity[:],
+                )
+            row[t] = held.tile([P, HALF], F32, name=f"row{t}")
+            nc.scalar.copy(row[t][:], spread[:])
 
-        half = LIST // 2
+        def bracket_and_rest(bracket, rest, b, g):
+            nc.scalar.activation(
+                bracket, b, ACT.Identity, bias=weight[:, 1, g : g + 1], scale=weight[:, 3, g : g + 1]
+            )
+            nc.scalar.activation(
+                rest, b, ACT.Identity, bias=weight[:, 0, g : g + 1], scale=weight[:, 2, g : g + 1]
+            )
+
         for r in range(ROW_BLOCKS):
-            n = LEVEL_GATES[0]
-            bracket = work.tile([P, n], F32, name="bracket")
+            rest1 = work.tile([P, HALF], F32, name="rest1")
             nc.vector.tensor_tensor(
-                bracket[:], windows[r][:].indirect(offsets[:, half // 16 :]), w3[:, :n], ALU.mult
+                rest1[:], windows[r][:].indirect(offsets[:, HALF // 16 :]), row[2][:], ALU.mult
             )
-            nc.vector.tensor_add(bracket[:], bracket[:], w1[:, :n])
-            rest = work.tile([P, n], F32, name="rest")
+            bracket1 = work.tile([P, HALF], F32, name="bracket1")
             nc.vector.tensor_tensor(
-                rest[:], windows[r][:].indirect(offsets[:, half // 16 :]), w2[:, :n], ALU.mult
+                bracket1[:], windows[r][:].indirect(offsets[:, HALF // 16 :]), row[3][:], ALU.mult
             )
-            nc.vector.tensor_add(rest[:], rest[:], w0[:, :n])
-            level = work.tile([P, n], F32, name="level")
+            nc.vector.tensor_add(bracket1[:], bracket1[:], row[1][:])
+            product1 = work.tile([P, HALF], F32, name="product1")
             nc.vector.tensor_tensor(
-                level[:], windows[r][:].indirect(offsets[:, : half // 16]), bracket[:], ALU.mult
+                product1[:], windows[r][:].indirect(offsets[:, : HALF // 16]), bracket1[:], ALU.mult
             )
-            nc.vector.tensor_add(level[:], level[:], rest[:])
 
-            lo = n
-            for n in LEVEL_GATES[1:]:
-                a, b = level[:, :n], level[:, n : 2 * n]
-                bracket = work.tile([P, n], F32, name="bracket")
-                nc.vector.tensor_mul(bracket[:], b, w3[:, lo : lo + n])
-                nc.vector.tensor_add(bracket[:], bracket[:], w1[:, lo : lo + n])
-                rest = work.tile([P, n], F32, name="rest")
-                nc.vector.tensor_mul(rest[:], b, w2[:, lo : lo + n])
-                nc.vector.tensor_add(rest[:], rest[:], w0[:, lo : lo + n])
-                level = work.tile([P, n], F32, name="level")
-                nc.vector.tensor_mul(level[:], a, bracket[:])
-                nc.vector.tensor_add(level[:], level[:], rest[:])
-                lo += n
+            level1 = psum.tile([P, HALF // P, P], F32, name="level1")
+            terms = (rest1, row[0], product1)
+            for i, term in enumerate(terms):
+                for g in range(HALF // P):
+                    add_flipped(
+                        level1[:, g, :],
+                        term[:, g * P : (g + 1) * P],
+                        start=(i == 0 and g == 0),
+                        stop=(i == len(terms) - 1 and g == HALF // P - 1),
+                    )
 
-            nc.sync.dma_start(out[r * P : (r + 1) * P, :], level[:])
+            bracket2 = work.tile([P, 2, P], F32, name="bracket2")
+            rest2 = work.tile([P, 2, P], F32, name="rest2")
+            for i in range(2):
+                bracket_and_rest(bracket2[:, i, :], rest2[:, i, :], level1[:, 2 + i, :], 4 + i)
+            level2 = work.tile([P, 2, P], F32, name="level2")
+            nc.vector.tensor_mul(level2[:], level1[:, 0:2, :], bracket2[:])
+            nc.vector.tensor_add(level2[:], level2[:], rest2[:])
+
+            bracket3 = work.tile([P, P], F32, name="bracket3")
+            rest3 = work.tile([P, P], F32, name="rest3")
+            bracket_and_rest(bracket3[:], rest3[:], level2[:, 1, :], 6)
+            product3 = work.tile([P, P], F32, name="product3")
+            nc.vector.tensor_mul(product3[:], level2[:, 0, :], bracket3[:])
+
+            level3 = psum.tile([P, P], F32, name="level3")
+            add_flipped(level3[:], rest3[:], start=True, stop=False)
+            add_flipped(level3[:], product3[:], start=False, stop=True)
+            result = work.tile([P, P], F32, name="result")
+            nc.scalar.copy(result[:], level3[:])
+            nc.sync.dma_start(out[r * P : (r + 1) * P, :], result[:])

@@ -105,7 +105,7 @@ def tile_logictreeconv2d_kernel(tc, x, logits, offs, out):
             nc.vector.tensor_tensor(
                 bracket1[:], windows[r][:].indirect(offsets[:, HALF // 16 :]), row[3][:], ALU.mult
             )
-            nc.vector.tensor_add(bracket1[:], bracket1[:], row[1][:])
+            nc.gpsimd.tensor_add(bracket1[:], bracket1[:], row[1][:])
             product1 = work.tile([P, HALF], F32, name="product1")
             nc.vector.tensor_tensor(
                 product1[:], windows[r][:].indirect(offsets[:, : HALF // 16]), bracket1[:], ALU.mult

@@ -12,6 +12,7 @@ ROWS, COLS = 512, 576
 ROW_BLOCKS = ROWS // P
 LIST = 1024
 HALF = LIST // 2
+PIECE = 256
 KINDS = 16
 GATE_BLOCKS = 7
 
@@ -27,7 +28,13 @@ def tile_logictreeconv2d_kernel(tc, x, logits, offs, out):
         nc.sync.dma_start(offsets[:], offs)
 
         kind_rows = held.tile([KINDS * GATE_BLOCKS, P], F32, name="kind_rows")
-        nc.scalar.dma_start(kind_rows[:], logits.rearrange("k (g n) -> (k g) n", n=P))
+        logit_rows = logits.rearrange("k (g n) -> (k g) n", n=P)
+        first = 0
+        for count in (64, 32, 16):
+            nc.scalar.dma_start(
+                kind_rows[first : first + count, :], logit_rows[first : first + count, :]
+            )
+            first += count
 
         windows = []
         for r in range(ROW_BLOCKS):
@@ -44,7 +51,7 @@ def tile_logictreeconv2d_kernel(tc, x, logits, offs, out):
                 acc, lhsT=term, rhs=identity[:], is_transpose=True, start=start, stop=stop
             )
 
-        flipped = psum.tile([P, KINDS * GATE_BLOCKS], F32, name="flipped", bufs=1)
+        flipped = psum.tile([P, KINDS * GATE_BLOCKS], F32, name="flipped", tag="spread")
         nc.tensor.transpose(
             flipped[:], kind_rows[:], identity[: KINDS * GATE_BLOCKS, : KINDS * GATE_BLOCKS]
         )
@@ -57,82 +64,94 @@ def tile_logictreeconv2d_kernel(tc, x, logits, offs, out):
             expo[:], by_kind, top[:].unsqueeze(1).to_broadcast([P, KINDS, GATE_BLOCKS])
         )
         nc.scalar.activation(expo[:], expo[:], ACT.Exp)
-        total = held.tile([P, GATE_BLOCKS], F32, name="total")
-        nc.vector.reduce_sum(total[:], expo[:].rearrange("p k g -> p g k"), axis=AXIS.X)
+        share = held.tile([P, 1, GATE_BLOCKS], F32, name="share")
+        nc.vector.reduce_sum(share[:, 0, :], expo[:].rearrange("p k g -> p g k"), axis=AXIS.X)
 
-        weight = held.tile([P, 4, GATE_BLOCKS], F32, name="weight")
+        corner = held.tile([P, 4, GATE_BLOCKS], F32, name="corner")
         for t, bit in enumerate((3, 1, 2, 0)):
             with_bit = expo[:].rearrange("p (hi two lo) g -> p two g hi lo", two=2, lo=2**bit)
-            nc.vector.reduce_sum(weight[:, t, :], with_bit[:, 1], axis=AXIS.XY)
-        nc.vector.reciprocal(total[:], total[:])
-        nc.vector.tensor_mul(
-            weight[:], weight[:], total[:].unsqueeze(1).to_broadcast([P, 4, GATE_BLOCKS])
-        )
-        nc.vector.tensor_sub(weight[:, 3, :], weight[:, 3, :], weight[:, 1, :])
+            nc.vector.reduce_sum(corner[:, t, :], with_bit[:, 1], axis=AXIS.XY)
+        nc.vector.reciprocal(share[:], share[:])
+
+        weight = held.tile([P, 4, GATE_BLOCKS], F32, name="weight")
         nc.vector.tensor_sub(
             weight[:, 1:3, :],
-            weight[:, 1:3, :],
-            weight[:, 0:1, :].to_broadcast([P, 2, GATE_BLOCKS]),
+            corner[:, 1:3, :],
+            corner[:, 0:1, :].to_broadcast([P, 2, GATE_BLOCKS]),
         )
+        nc.vector.tensor_sub(corner[:, 3, :], corner[:, 3, :], corner[:, 1, :])
+        nc.vector.tensor_mul(
+            weight[:, 1:3, :], weight[:, 1:3, :], share[:].to_broadcast([P, 2, GATE_BLOCKS])
+        )
+        nc.vector.tensor_mul(weight[:, 3, :], corner[:, 3, :], share[:, 0, :])
         nc.vector.tensor_sub(weight[:, 3, :], weight[:, 3, :], weight[:, 2, :])
+        nc.vector.tensor_mul(weight[:, 0, :], corner[:, 0, :], share[:, 0, :])
 
-        row = {}
+        row = {t: held.tile([P, HALF], F32, name=f"row{t}") for t in range(4)}
         for t in (2, 3, 1, 0):
-            spread = psum.tile([P, HALF], F32, name="spread")
-            for g in range(HALF // P):
-                nc.tensor.transpose(
-                    spread[:, g * P : (g + 1) * P],
-                    weight[:, t, g : g + 1].to_broadcast([P, P]),
-                    identity[:],
-                )
-            row[t] = held.tile([P, HALF], F32, name=f"row{t}")
-            nc.scalar.copy(row[t][:], spread[:])
+            for h in range(HALF // PIECE):
+                spread = psum.tile([P, PIECE], F32, name="spread")
+                for i in range(PIECE // P):
+                    g = h * (PIECE // P) + i
+                    nc.tensor.transpose(
+                        spread[:, i * P : (i + 1) * P],
+                        weight[:, t, g : g + 1].to_broadcast([P, P]),
+                        identity[:],
+                    )
+                nc.scalar.copy(row[t][:, h * PIECE : (h + 1) * PIECE], spread[:])
 
-        def bracket_and_rest(bracket, rest, b, g):
+        def affine(result, b, g, t_bias, t_scale):
             nc.scalar.activation(
-                bracket, b, ACT.Identity, bias=weight[:, 1, g : g + 1], scale=weight[:, 3, g : g + 1]
-            )
-            nc.scalar.activation(
-                rest, b, ACT.Identity, bias=weight[:, 0, g : g + 1], scale=weight[:, 2, g : g + 1]
+                result,
+                b,
+                ACT.Identity,
+                bias=weight[:, t_bias, g : g + 1],
+                scale=weight[:, t_scale, g : g + 1],
             )
 
         for r in range(ROW_BLOCKS):
+            list_a = offsets[:, : HALF // 16]
+            list_b = offsets[:, HALF // 16 :]
             rest1 = work.tile([P, HALF], F32, name="rest1")
-            nc.vector.tensor_tensor(
-                rest1[:], windows[r][:].indirect(offsets[:, HALF // 16 :]), row[2][:], ALU.mult
-            )
+            nc.vector.tensor_tensor(rest1[:], windows[r][:].indirect(list_b), row[2][:], ALU.mult)
             bracket1 = work.tile([P, HALF], F32, name="bracket1")
             nc.vector.tensor_tensor(
-                bracket1[:], windows[r][:].indirect(offsets[:, HALF // 16 :]), row[3][:], ALU.mult
+                bracket1[:], windows[r][:].indirect(list_b), row[3][:], ALU.mult
             )
-            nc.gpsimd.tensor_add(bracket1[:], bracket1[:], row[1][:])
+            nc.vector.tensor_add(bracket1[:], bracket1[:], row[1][:])
             product1 = work.tile([P, HALF], F32, name="product1")
             nc.vector.tensor_tensor(
-                product1[:], windows[r][:].indirect(offsets[:, : HALF // 16]), bracket1[:], ALU.mult
+                product1[:], windows[r][:].indirect(list_a), bracket1[:], ALU.mult
             )
 
-            level1 = psum.tile([P, HALF // P, P], F32, name="level1")
+            level1 = {}
             terms = (rest1, row[0], product1)
-            for i, term in enumerate(terms):
-                for g in range(HALF // P):
-                    add_flipped(
-                        level1[:, g, :],
-                        term[:, g * P : (g + 1) * P],
-                        start=(i == 0 and g == 0),
-                        stop=(i == len(terms) - 1 and g == HALF // P - 1),
-                    )
+            for h in (1, 0):
+                level1[h] = psum.tile([P, PIECE // P, P], F32, name=f"level1_{h}")
+                for n, term in enumerate(terms):
+                    for i in range(PIECE // P):
+                        g = h * (PIECE // P) + i
+                        add_flipped(
+                            level1[h][:, i, :],
+                            term[:, g * P : (g + 1) * P],
+                            start=(n == 0 and i == 0),
+                            stop=(n == len(terms) - 1 and i == PIECE // P - 1),
+                        )
 
             bracket2 = work.tile([P, 2, P], F32, name="bracket2")
             rest2 = work.tile([P, 2, P], F32, name="rest2")
             for i in range(2):
-                bracket_and_rest(bracket2[:, i, :], rest2[:, i, :], level1[:, 2 + i, :], 4 + i)
+                affine(bracket2[:, i, :], level1[1][:, i, :], 4 + i, 1, 3)
+            for i in range(2):
+                affine(rest2[:, i, :], level1[1][:, i, :], 4 + i, 0, 2)
             level2 = work.tile([P, 2, P], F32, name="level2")
-            nc.vector.tensor_mul(level2[:], level1[:, 0:2, :], bracket2[:])
+            nc.vector.tensor_mul(level2[:], level1[0][:], bracket2[:])
             nc.vector.tensor_add(level2[:], level2[:], rest2[:])
 
             bracket3 = work.tile([P, P], F32, name="bracket3")
             rest3 = work.tile([P, P], F32, name="rest3")
-            bracket_and_rest(bracket3[:], rest3[:], level2[:, 1, :], 6)
+            affine(bracket3[:], level2[:, 1, :], 6, 1, 3)
+            affine(rest3[:], level2[:, 1, :], 6, 0, 2)
             product3 = work.tile([P, P], F32, name="product3")
             nc.vector.tensor_mul(product3[:], level2[:, 0, :], bracket3[:])
 

@@ -28,13 +28,7 @@ def tile_logictreeconv2d_kernel(tc, x, logits, offs, out):
         nc.sync.dma_start(offsets[:], offs)
 
         kind_rows = held.tile([KINDS * GATE_BLOCKS, P], F32, name="kind_rows")
-        logit_rows = logits.rearrange("k (g n) -> (k g) n", n=P)
-        first = 0
-        for count in (64, 32, 16):
-            nc.scalar.dma_start(
-                kind_rows[first : first + count, :], logit_rows[first : first + count, :]
-            )
-            first += count
+        nc.scalar.dma_start(kind_rows[:], logits.rearrange("k (g n) -> (k g) n", n=P))
 
         windows = []
         for r in range(ROW_BLOCKS):

@@ -8,13 +8,14 @@ ACT = mybir.ActivationFunctionType
 AXIS = mybir.AxisListType
 
 P = 128
-ROWS, COLS = 512, 576
-ROW_BLOCKS = ROWS // P
+POSITIONS, ENTRIES = 512, 576
+POSITION_BLOCKS = POSITIONS // P
 LIST = 1024
-HALF = LIST // 2
-PIECE = 256
+LEVEL1 = LIST // 2
+HALF1 = LEVEL1 // 2
 KINDS = 16
 GATE_BLOCKS = 7
+LEVEL2_BLOCK, LEVEL3_BLOCK = 4, 6
 
 
 def tile_logictreeconv2d_kernel(tc, x, logits, offs, out):
@@ -24,15 +25,17 @@ def tile_logictreeconv2d_kernel(tc, x, logits, offs, out):
         tc.tile_pool(name="work", bufs=3) as work,
         tc.psum_pool(name="psum", bufs=2) as psum,
     ):
+        kind_rows = held.tile([KINDS * GATE_BLOCKS, P], F32, name="kind_rows")
+        nc.sync.dma_start(kind_rows[:], logits.rearrange("k (g n) -> (k g) n", n=P))
+
         offsets = held.tile([P, LIST // 16], U16, name="offsets")
         nc.sync.dma_start(offsets[:], offs)
-
-        kind_rows = held.tile([KINDS * GATE_BLOCKS, P], F32, name="kind_rows")
-        nc.scalar.dma_start(kind_rows[:], logits.rearrange("k (g n) -> (k g) n", n=P))
+        list_a = offsets[:, : LEVEL1 // 16]
+        list_b = offsets[:, LEVEL1 // 16 :]
 
         windows = []
-        for r in range(ROW_BLOCKS):
-            window = held.tile([P, COLS], F32, name=f"window{r}")
+        for r in range(POSITION_BLOCKS):
+            window = held.tile([P, ENTRIES], F32, name=f"window{r}")
             queue = nc.sync if r % 2 == 0 else nc.scalar
             queue.dma_start(window[:], x[r * P : (r + 1) * P, :])
             windows.append(window)
@@ -40,32 +43,34 @@ def tile_logictreeconv2d_kernel(tc, x, logits, offs, out):
         identity = held.tile([P, P], F32, name="identity")
         make_identity(nc, identity[:])
 
-        def add_flipped(acc, term, start, stop):
+        def add_turned(bank, block, start, stop):
             nc.tensor.matmul(
-                acc, lhsT=term, rhs=identity[:], is_transpose=True, start=start, stop=stop
+                bank, lhsT=block, rhs=identity[:], is_transpose=True, start=start, stop=stop
             )
 
-        flipped = psum.tile([P, KINDS * GATE_BLOCKS], F32, name="flipped", tag="spread")
+        gate_kinds = psum.tile([P, KINDS * GATE_BLOCKS], F32, name="gate_kinds", tag="row_piece")
         nc.tensor.transpose(
-            flipped[:], kind_rows[:], identity[: KINDS * GATE_BLOCKS, : KINDS * GATE_BLOCKS]
+            gate_kinds[:], kind_rows[:], identity[: KINDS * GATE_BLOCKS, : KINDS * GATE_BLOCKS]
         )
-        by_kind = flipped[:].rearrange("p (k g) -> p k g", g=GATE_BLOCKS)
+        by_kind = gate_kinds[:].rearrange("p (k g) -> p k g", g=GATE_BLOCKS)
 
-        top = held.tile([P, GATE_BLOCKS], F32, name="top")
-        nc.vector.reduce_max(top[:], by_kind.rearrange("p k g -> p g k"), axis=AXIS.X)
-        expo = held.tile([P, KINDS, GATE_BLOCKS], F32, name="expo")
+        largest = held.tile([P, GATE_BLOCKS], F32, name="largest")
+        nc.vector.reduce_max(largest[:], by_kind.rearrange("p k g -> p g k"), axis=AXIS.X)
+        exps = held.tile([P, KINDS, GATE_BLOCKS], F32, name="exps")
         nc.vector.tensor_sub(
-            expo[:], by_kind, top[:].unsqueeze(1).to_broadcast([P, KINDS, GATE_BLOCKS])
+            exps[:], by_kind, largest[:].unsqueeze(1).to_broadcast([P, KINDS, GATE_BLOCKS])
         )
-        nc.scalar.activation(expo[:], expo[:], ACT.Exp)
-        share = held.tile([P, 1, GATE_BLOCKS], F32, name="share")
-        nc.vector.reduce_sum(share[:, 0, :], expo[:].rearrange("p k g -> p g k"), axis=AXIS.X)
+        nc.scalar.activation(exps[:], exps[:], ACT.Exp)
+        inverse_sum = held.tile([P, 1, GATE_BLOCKS], F32, name="inverse_sum")
+        nc.vector.reduce_sum(
+            inverse_sum[:, 0, :], exps[:].rearrange("p k g -> p g k"), axis=AXIS.X
+        )
 
         corner = held.tile([P, 4, GATE_BLOCKS], F32, name="corner")
-        for t, bit in enumerate((3, 1, 2, 0)):
-            with_bit = expo[:].rearrange("p (hi two lo) g -> p two g hi lo", two=2, lo=2**bit)
-            nc.vector.reduce_sum(corner[:, t, :], with_bit[:, 1], axis=AXIS.XY)
-        nc.vector.reciprocal(share[:], share[:])
+        for place, bit in enumerate((3, 1, 2, 0)):
+            with_bit = exps[:].rearrange("p (hi two lo) g -> p two g hi lo", two=2, lo=2**bit)
+            nc.vector.reduce_sum(corner[:, place, :], with_bit[:, 1], axis=AXIS.XY)
+        nc.vector.reciprocal(inverse_sum[:], inverse_sum[:])
 
         weight = held.tile([P, 4, GATE_BLOCKS], F32, name="weight")
         nc.vector.tensor_sub(
@@ -75,45 +80,43 @@ def tile_logictreeconv2d_kernel(tc, x, logits, offs, out):
         )
         nc.vector.tensor_sub(corner[:, 3, :], corner[:, 3, :], corner[:, 1, :])
         nc.vector.tensor_mul(
-            weight[:, 1:3, :], weight[:, 1:3, :], share[:].to_broadcast([P, 2, GATE_BLOCKS])
+            weight[:, 1:3, :], weight[:, 1:3, :], inverse_sum[:].to_broadcast([P, 2, GATE_BLOCKS])
         )
-        nc.vector.tensor_mul(weight[:, 3, :], corner[:, 3, :], share[:, 0, :])
+        nc.vector.tensor_mul(weight[:, 3, :], corner[:, 3, :], inverse_sum[:, 0, :])
         nc.vector.tensor_sub(weight[:, 3, :], weight[:, 3, :], weight[:, 2, :])
-        nc.vector.tensor_mul(weight[:, 0, :], corner[:, 0, :], share[:, 0, :])
+        nc.vector.tensor_mul(weight[:, 0, :], corner[:, 0, :], inverse_sum[:, 0, :])
 
-        row = {t: held.tile([P, HALF], F32, name=f"row{t}") for t in range(4)}
+        row = {t: held.tile([P, LEVEL1], F32, name=f"row{t}") for t in range(4)}
         for t in (2, 3, 1, 0):
-            for h in range(HALF // PIECE):
-                spread = psum.tile([P, PIECE], F32, name="spread")
-                for i in range(PIECE // P):
-                    g = h * (PIECE // P) + i
+            for h in range(LEVEL1 // HALF1):
+                row_piece = psum.tile([P, HALF1], F32, name="row_piece")
+                for i in range(HALF1 // P):
+                    g = h * (HALF1 // P) + i
                     nc.tensor.transpose(
-                        spread[:, i * P : (i + 1) * P],
+                        row_piece[:, i * P : (i + 1) * P],
                         weight[:, t, g : g + 1].to_broadcast([P, P]),
                         identity[:],
                     )
-                nc.scalar.copy(row[t][:, h * PIECE : (h + 1) * PIECE], spread[:])
+                nc.scalar.copy(row[t][:, h * HALF1 : (h + 1) * HALF1], row_piece[:])
 
-        def affine(result, b, g, t_bias, t_scale):
+        def affine(dest, b, g, t_bias, t_scale):
             nc.scalar.activation(
-                result,
+                dest,
                 b,
                 ACT.Identity,
                 bias=weight[:, t_bias, g : g + 1],
                 scale=weight[:, t_scale, g : g + 1],
             )
 
-        for r in range(ROW_BLOCKS):
-            list_a = offsets[:, : HALF // 16]
-            list_b = offsets[:, HALF // 16 :]
-            rest1 = work.tile([P, HALF], F32, name="rest1")
+        for r in range(POSITION_BLOCKS):
+            rest1 = work.tile([P, LEVEL1], F32, name="rest1")
             nc.vector.tensor_tensor(rest1[:], windows[r][:].indirect(list_b), row[2][:], ALU.mult)
-            bracket1 = work.tile([P, HALF], F32, name="bracket1")
+            bracket1 = work.tile([P, LEVEL1], F32, name="bracket1")
             nc.vector.tensor_tensor(
                 bracket1[:], windows[r][:].indirect(list_b), row[3][:], ALU.mult
             )
             nc.vector.tensor_add(bracket1[:], bracket1[:], row[1][:])
-            product1 = work.tile([P, HALF], F32, name="product1")
+            product1 = work.tile([P, LEVEL1], F32, name="product1")
             nc.vector.tensor_tensor(
                 product1[:], windows[r][:].indirect(list_a), bracket1[:], ALU.mult
             )
@@ -121,37 +124,37 @@ def tile_logictreeconv2d_kernel(tc, x, logits, offs, out):
             level1 = {}
             terms = (rest1, row[0], product1)
             for h in (1, 0):
-                level1[h] = psum.tile([P, PIECE // P, P], F32, name=f"level1_{h}")
-                for n, term in enumerate(terms):
-                    for i in range(PIECE // P):
-                        g = h * (PIECE // P) + i
-                        add_flipped(
+                level1[h] = psum.tile([P, HALF1 // P, P], F32, name=f"level1_{h}")
+                for which, term in enumerate(terms):
+                    for i in range(HALF1 // P):
+                        g = h * (HALF1 // P) + i
+                        add_turned(
                             level1[h][:, i, :],
                             term[:, g * P : (g + 1) * P],
-                            start=(n == 0 and i == 0),
-                            stop=(n == len(terms) - 1 and i == PIECE // P - 1),
+                            start=(which == 0 and i == 0),
+                            stop=(which == len(terms) - 1 and i == HALF1 // P - 1),
                         )
 
             bracket2 = work.tile([P, 2, P], F32, name="bracket2")
             rest2 = work.tile([P, 2, P], F32, name="rest2")
             for i in range(2):
-                affine(bracket2[:, i, :], level1[1][:, i, :], 4 + i, 1, 3)
+                affine(bracket2[:, i, :], level1[1][:, i, :], LEVEL2_BLOCK + i, t_bias=1, t_scale=3)
             for i in range(2):
-                affine(rest2[:, i, :], level1[1][:, i, :], 4 + i, 0, 2)
+                affine(rest2[:, i, :], level1[1][:, i, :], LEVEL2_BLOCK + i, t_bias=0, t_scale=2)
             level2 = work.tile([P, 2, P], F32, name="level2")
             nc.vector.tensor_mul(level2[:], level1[0][:], bracket2[:])
             nc.vector.tensor_add(level2[:], level2[:], rest2[:])
 
             bracket3 = work.tile([P, P], F32, name="bracket3")
             rest3 = work.tile([P, P], F32, name="rest3")
-            affine(bracket3[:], level2[:, 1, :], 6, 1, 3)
-            affine(rest3[:], level2[:, 1, :], 6, 0, 2)
+            affine(bracket3[:], level2[:, 1, :], LEVEL3_BLOCK, t_bias=1, t_scale=3)
+            affine(rest3[:], level2[:, 1, :], LEVEL3_BLOCK, t_bias=0, t_scale=2)
             product3 = work.tile([P, P], F32, name="product3")
             nc.vector.tensor_mul(product3[:], level2[:, 0, :], bracket3[:])
 
             level3 = psum.tile([P, P], F32, name="level3")
-            add_flipped(level3[:], rest3[:], start=True, stop=False)
-            add_flipped(level3[:], product3[:], start=False, stop=True)
-            result = work.tile([P, P], F32, name="result")
-            nc.scalar.copy(result[:], level3[:])
-            nc.sync.dma_start(out[r * P : (r + 1) * P, :], result[:])
+            add_turned(level3[:], rest3[:], start=True, stop=False)
+            add_turned(level3[:], product3[:], start=False, stop=True)
+            channels = work.tile([P, P], F32, name="channels")
+            nc.scalar.copy(channels[:], level3[:])
+            nc.sync.dma_start(out[r * P : (r + 1) * P, :], channels[:])

@@ -12,6 +12,7 @@ POSITIONS, ENTRIES = 512, 576
 POSITION_BLOCKS = POSITIONS // P
 LIST = 1024
 LEVEL1 = LIST // 2
+LEVEL1_BLOCKS = LEVEL1 // P
 HALF1 = LEVEL1 // 2
 KINDS = 16
 GATE_BLOCKS = 7
@@ -22,8 +23,9 @@ def tile_logictreeconv2d_kernel(tc, x, logits, offs, out):
     nc = tc.nc
     with (
         tc.tile_pool(name="held", bufs=1) as held,
-        tc.tile_pool(name="work", bufs=3) as work,
-        tc.psum_pool(name="psum", bufs=2) as psum,
+        tc.tile_pool(name="work", bufs=POSITION_BLOCKS) as work,
+        tc.psum_pool(name="psum_whole", bufs=2) as psum_whole,
+        tc.psum_pool(name="psum_part", bufs=4) as psum_part,
     ):
         kind_rows = held.tile([KINDS * GATE_BLOCKS, P], F32, name="kind_rows")
         nc.sync.dma_start(kind_rows[:], logits.rearrange("k (g n) -> (k g) n", n=P))
@@ -48,7 +50,21 @@ def tile_logictreeconv2d_kernel(tc, x, logits, offs, out):
                 bank, lhsT=block, rhs=identity[:], is_transpose=True, start=start, stop=stop
             )
 
-        gate_kinds = psum.tile([P, KINDS * GATE_BLOCKS], F32, name="gate_kinds", tag="row_piece")
+        def spread(columns, name):
+            row = held.tile([P, LEVEL1], F32, name=name)
+            for h in range(LEVEL1 // HALF1):
+                piece = psum_part.tile([P, HALF1], F32, name="piece", tag="part")
+                for i in range(HALF1 // P):
+                    g = h * (HALF1 // P) + i
+                    nc.tensor.transpose(
+                        piece[:, i * P : (i + 1) * P],
+                        columns[:, g : g + 1].to_broadcast([P, P]),
+                        identity[:],
+                    )
+                nc.scalar.copy(row[:, h * HALF1 : (h + 1) * HALF1], piece[:])
+            return row
+
+        gate_kinds = psum_whole.tile([P, KINDS * GATE_BLOCKS], F32, name="gate_kinds", tag="turned")
         nc.tensor.transpose(
             gate_kinds[:], kind_rows[:], identity[: KINDS * GATE_BLOCKS, : KINDS * GATE_BLOCKS]
         )
@@ -65,66 +81,73 @@ def tile_logictreeconv2d_kernel(tc, x, logits, offs, out):
         nc.vector.reduce_sum(
             inverse_sum[:, 0, :], exps[:].rearrange("p k g -> p g k"), axis=AXIS.X
         )
-
-        corner = held.tile([P, 4, GATE_BLOCKS], F32, name="corner")
-        for place, bit in enumerate((3, 1, 2, 0)):
-            with_bit = exps[:].rearrange("p (hi two lo) g -> p two g hi lo", two=2, lo=2**bit)
-            nc.vector.reduce_sum(corner[:, place, :], with_bit[:, 1], axis=AXIS.XY)
         nc.vector.reciprocal(inverse_sum[:], inverse_sum[:])
 
-        weight = held.tile([P, 4, GATE_BLOCKS], F32, name="weight")
+        inverse_row = spread(inverse_sum[:, 0, :], "inverse_row")
+
+        raw = held.tile([P, 4, GATE_BLOCKS], F32, name="raw")
+        for place, bit in enumerate((3, 1, 2, 0)):
+            with_bit = exps[:].rearrange("p (hi two lo) g -> p two g hi lo", two=2, lo=2**bit)
+            nc.vector.reduce_sum(raw[:, place, :], with_bit[:, 1], axis=AXIS.XY)
+
+        nc.vector.tensor_sub(raw[:, 3, :], raw[:, 3, :], raw[:, 1, :])
         nc.vector.tensor_sub(
-            weight[:, 1:3, :],
-            corner[:, 1:3, :],
-            corner[:, 0:1, :].to_broadcast([P, 2, GATE_BLOCKS]),
+            raw[:, 1:3, :], raw[:, 1:3, :], raw[:, 0:1, :].to_broadcast([P, 2, GATE_BLOCKS])
         )
-        nc.vector.tensor_sub(corner[:, 3, :], corner[:, 3, :], corner[:, 1, :])
-        nc.vector.tensor_mul(
-            weight[:, 1:3, :], weight[:, 1:3, :], inverse_sum[:].to_broadcast([P, 2, GATE_BLOCKS])
-        )
-        nc.vector.tensor_mul(weight[:, 3, :], corner[:, 3, :], inverse_sum[:, 0, :])
-        nc.vector.tensor_sub(weight[:, 3, :], weight[:, 3, :], weight[:, 2, :])
-        nc.vector.tensor_mul(weight[:, 0, :], corner[:, 0, :], inverse_sum[:, 0, :])
+        nc.vector.tensor_sub(raw[:, 3, :], raw[:, 3, :], raw[:, 2, :])
+        weight = held.tile([P, 4, GATE_BLOCKS], F32, name="weight")
+        nc.vector.tensor_mul(weight[:], raw[:], inverse_sum[:].to_broadcast([P, 4, GATE_BLOCKS]))
 
-        row = {t: held.tile([P, LEVEL1], F32, name=f"row{t}") for t in range(4)}
-        for t in (2, 3, 1, 0):
-            for h in range(LEVEL1 // HALF1):
-                row_piece = psum.tile([P, HALF1], F32, name="row_piece")
-                for i in range(HALF1 // P):
-                    g = h * (HALF1 // P) + i
-                    nc.tensor.transpose(
-                        row_piece[:, i * P : (i + 1) * P],
-                        weight[:, t, g : g + 1].to_broadcast([P, P]),
-                        identity[:],
-                    )
-                nc.scalar.copy(row[t][:, h * HALF1 : (h + 1) * HALF1], row_piece[:])
+        raw2_row = spread(raw[:, 2, :], "raw2_row")
+        weight0_row = spread(weight[:, 0, :], "weight0_row")
 
-        def affine(dest, b, g, t_bias, t_scale):
-            nc.scalar.activation(
-                dest,
-                b,
-                ACT.Identity,
-                bias=weight[:, t_bias, g : g + 1],
-                scale=weight[:, t_scale, g : g + 1],
-            )
+        def affine(dest, b, bias, scale):
+            nc.scalar.activation(dest, b, ACT.Identity, bias=bias, scale=scale)
 
-        for r in range(POSITION_BLOCKS):
-            rest1 = work.tile([P, LEVEL1], F32, name="rest1")
-            nc.vector.tensor_tensor(rest1[:], windows[r][:].indirect(list_b), row[2][:], ALU.mult)
-            bracket1 = work.tile([P, LEVEL1], F32, name="bracket1")
+        def bracket_of(dest, b, g):
+            affine(dest, b, bias=weight[:, 1, g : g + 1], scale=weight[:, 3, g : g + 1])
+
+        def rest_of(dest, b, g):
+            affine(dest, b, bias=weight[:, 0, g : g + 1], scale=weight[:, 2, g : g + 1])
+
+        kept = {}
+
+        def pick_b(r):
+            scaled_b = work.tile([P, LEVEL1], F32, name="scaled_b")
             nc.vector.tensor_tensor(
-                bracket1[:], windows[r][:].indirect(list_b), row[3][:], ALU.mult
+                scaled_b[:], windows[r][:].indirect(list_b), inverse_row[:], ALU.mult
             )
-            nc.vector.tensor_add(bracket1[:], bracket1[:], row[1][:])
+            turned = psum_whole.tile([P, LEVEL1_BLOCKS, P], F32, name="turned")
+            for g in range(LEVEL1_BLOCKS):
+                nc.tensor.transpose(turned[:, g, :], scaled_b[:, g * P : (g + 1) * P], identity[:])
+            bracket_turned = work.tile([P, LEVEL1_BLOCKS, P], F32, name="bracket_turned")
+            for g in range(LEVEL1_BLOCKS):
+                affine(
+                    bracket_turned[:, g, :],
+                    turned[:, g, :],
+                    bias=weight[:, 1, g : g + 1],
+                    scale=raw[:, 3, g : g + 1],
+                )
+            turned_back = psum_whole.tile([P, LEVEL1], F32, name="turned_back")
+            for g in range(LEVEL1_BLOCKS):
+                nc.tensor.transpose(
+                    turned_back[:, g * P : (g + 1) * P], bracket_turned[:, g, :], identity[:]
+                )
+            bracket1 = work.tile([P, LEVEL1], F32, name="bracket1")
+            nc.scalar.copy(bracket1[:], turned_back[:])
+            rest1 = work.tile([P, LEVEL1], F32, name="rest1")
+            nc.vector.tensor_mul(rest1[:], scaled_b[:], raw2_row[:])
+            kept["bracket1", r], kept["rest1", r] = bracket1, rest1
+
+        def pick_a(r):
             product1 = work.tile([P, LEVEL1], F32, name="product1")
             nc.vector.tensor_tensor(
-                product1[:], windows[r][:].indirect(list_a), bracket1[:], ALU.mult
+                product1[:], windows[r][:].indirect(list_a), kept["bracket1", r][:], ALU.mult
             )
-
             level1 = {}
-            terms = (rest1, row[0], product1)
+            terms = (kept["rest1", r], weight0_row, product1)
             for h in (1, 0):
-                level1[h] = psum.tile([P, HALF1 // P, P], F32, name=f"level1_{h}")
+                level1[h] = psum_part.tile([P, HALF1 // P, P], F32, name=f"level1_{h}", tag="part")
                 for which, term in enumerate(terms):
                     for i in range(HALF1 // P):
                         g = h * (HALF1 // P) + i
@@ -134,27 +157,36 @@ def tile_logictreeconv2d_kernel(tc, x, logits, offs, out):
                             start=(which == 0 and i == 0),
                             stop=(which == len(terms) - 1 and i == HALF1 // P - 1),
                         )
-
             bracket2 = work.tile([P, 2, P], F32, name="bracket2")
             rest2 = work.tile([P, 2, P], F32, name="rest2")
             for i in range(2):
-                affine(bracket2[:, i, :], level1[1][:, i, :], LEVEL2_BLOCK + i, t_bias=1, t_scale=3)
+                bracket_of(bracket2[:, i, :], level1[1][:, i, :], LEVEL2_BLOCK + i)
             for i in range(2):
-                affine(rest2[:, i, :], level1[1][:, i, :], LEVEL2_BLOCK + i, t_bias=0, t_scale=2)
-            level2 = work.tile([P, 2, P], F32, name="level2")
-            nc.vector.tensor_mul(level2[:], level1[0][:], bracket2[:])
-            nc.vector.tensor_add(level2[:], level2[:], rest2[:])
+                rest_of(rest2[:, i, :], level1[1][:, i, :], LEVEL2_BLOCK + i)
+            kept["level1_a", r], kept["bracket2", r], kept["rest2", r] = level1[0], bracket2, rest2
 
+        def level_2(r):
+            level2 = work.tile([P, 2, P], F32, name="level2")
+            nc.vector.tensor_mul(level2[:], kept["level1_a", r][:], kept["bracket2", r][:])
+            nc.vector.tensor_add(level2[:], level2[:], kept["rest2", r][:])
             bracket3 = work.tile([P, P], F32, name="bracket3")
             rest3 = work.tile([P, P], F32, name="rest3")
-            affine(bracket3[:], level2[:, 1, :], LEVEL3_BLOCK, t_bias=1, t_scale=3)
-            affine(rest3[:], level2[:, 1, :], LEVEL3_BLOCK, t_bias=0, t_scale=2)
-            product3 = work.tile([P, P], F32, name="product3")
-            nc.vector.tensor_mul(product3[:], level2[:, 0, :], bracket3[:])
+            bracket_of(bracket3[:], level2[:, 1, :], LEVEL3_BLOCK)
+            rest_of(rest3[:], level2[:, 1, :], LEVEL3_BLOCK)
+            kept["level2", r], kept["bracket3", r], kept["rest3", r] = level2, bracket3, rest3
 
-            level3 = psum.tile([P, P], F32, name="level3")
-            add_turned(level3[:], rest3[:], start=True, stop=False)
+        def level_3(r):
+            product3 = work.tile([P, P], F32, name="product3")
+            nc.vector.tensor_mul(product3[:], kept["level2", r][:, 0, :], kept["bracket3", r][:])
+            level3 = psum_part.tile([P, P], F32, name="level3", tag="part")
+            add_turned(level3[:], kept["rest3", r][:], start=True, stop=False)
             add_turned(level3[:], product3[:], start=False, stop=True)
             channels = work.tile([P, P], F32, name="channels")
             nc.scalar.copy(channels[:], level3[:])
             nc.sync.dma_start(out[r * P : (r + 1) * P, :], channels[:])
+
+        stages = ((pick_b, 0), (pick_a, 2), (level_2, 3), (level_3, 4))
+        for step in range(POSITION_BLOCKS + stages[-1][1]):
+            for stage, lag in stages:
+                if 0 <= step - lag < POSITION_BLOCKS:
+                    stage(step - lag)

@@ -128,24 +128,29 @@ def tile_logictreeconv2d_kernel(tc, x, logits, offs, out):
                     bias=weight[:, 1, g : g + 1],
                     scale=raw[:, 3, g : g + 1],
                 )
+            kept["scaled_b", r], kept["bracket_turned", r] = scaled_b, bracket_turned
+
+        def turn_back(r):
             turned_back = psum_whole.tile([P, LEVEL1], F32, name="turned_back")
             for g in range(LEVEL1_BLOCKS):
                 nc.tensor.transpose(
-                    turned_back[:, g * P : (g + 1) * P], bracket_turned[:, g, :], identity[:]
+                    turned_back[:, g * P : (g + 1) * P],
+                    kept["bracket_turned", r][:, g, :],
+                    identity[:],
                 )
             bracket1 = work.tile([P, LEVEL1], F32, name="bracket1")
             nc.scalar.copy(bracket1[:], turned_back[:])
-            rest1 = work.tile([P, LEVEL1], F32, name="rest1")
-            nc.vector.tensor_mul(rest1[:], scaled_b[:], raw2_row[:])
-            kept["bracket1", r], kept["rest1", r] = bracket1, rest1
+            kept["bracket1", r] = bracket1
 
         def pick_a(r):
+            rest1 = work.tile([P, LEVEL1], F32, name="rest1")
+            nc.vector.tensor_mul(rest1[:], kept["scaled_b", r][:], raw2_row[:])
             product1 = work.tile([P, LEVEL1], F32, name="product1")
             nc.vector.tensor_tensor(
                 product1[:], windows[r][:].indirect(list_a), kept["bracket1", r][:], ALU.mult
             )
             level1 = {}
-            terms = (kept["rest1", r], weight0_row, product1)
+            terms = (rest1, weight0_row, product1)
             for h in (1, 0):
                 level1[h] = psum_part.tile([P, HALF1 // P, P], F32, name=f"level1_{h}", tag="part")
                 for which, term in enumerate(terms):
@@ -185,8 +190,8 @@ def tile_logictreeconv2d_kernel(tc, x, logits, offs, out):
             nc.scalar.copy(channels[:], level3[:])
             nc.sync.dma_start(out[r * P : (r + 1) * P, :], channels[:])
 
-        stages = ((pick_b, 0), (pick_a, 2), (level_2, 3), (level_3, 4))
-        for step in range(POSITION_BLOCKS + stages[-1][1]):
+        stages = ((pick_b, 0), (pick_a, 3), (turn_back, 1), (level_2, 4), (level_3, 5))
+        for step in range(POSITION_BLOCKS + max(lag for stage, lag in stages)):
             for stage, lag in stages:
                 if 0 <= step - lag < POSITION_BLOCKS:
                     stage(step - lag)

@@ -24,8 +24,8 @@ def tile_logictreeconv2d_kernel(tc, x, logits, offs, out):
     with (
         tc.tile_pool(name="held", bufs=1) as held,
         tc.tile_pool(name="work", bufs=POSITION_BLOCKS) as work,
-        tc.psum_pool(name="psum_whole", bufs=2) as psum_whole,
-        tc.psum_pool(name="psum_part", bufs=4) as psum_part,
+        tc.psum_pool(name="psum_whole", bufs=1) as psum_whole,
+        tc.psum_pool(name="psum_part", bufs=6) as psum_part,
     ):
         kind_rows = held.tile([KINDS * GATE_BLOCKS, P], F32, name="kind_rows")
         nc.sync.dma_start(kind_rows[:], logits.rearrange("k (g n) -> (k g) n", n=P))
@@ -190,7 +190,7 @@ def tile_logictreeconv2d_kernel(tc, x, logits, offs, out):
             nc.scalar.copy(channels[:], level3[:])
             nc.sync.dma_start(out[r * P : (r + 1) * P, :], channels[:])
 
-        stages = ((pick_b, 0), (pick_a, 3), (turn_back, 1), (level_2, 4), (level_3, 5))
+        stages = ((pick_b, 0), (pick_a, 3), (turn_back, 1), (level_2, 5), (level_3, 6))
         for step in range(POSITION_BLOCKS + max(lag for stage, lag in stages)):
             for stage, lag in stages:
                 if 0 <= step - lag < POSITION_BLOCKS:

@@ -142,15 +142,18 @@ def tile_logictreeconv2d_kernel(tc, x, logits, offs, out):
             nc.scalar.copy(bracket1[:], turned_back[:])
             kept["bracket1", r] = bracket1
 
-        def pick_a(r):
+        def rest_1(r):
             rest1 = work.tile([P, LEVEL1], F32, name="rest1")
             nc.vector.tensor_mul(rest1[:], kept["scaled_b", r][:], raw2_row[:])
+            kept["rest1", r] = rest1
+
+        def pick_a(r):
             product1 = work.tile([P, LEVEL1], F32, name="product1")
             nc.vector.tensor_tensor(
                 product1[:], windows[r][:].indirect(list_a), kept["bracket1", r][:], ALU.mult
             )
             level1 = {}
-            terms = (rest1, weight0_row, product1)
+            terms = (kept["rest1", r], weight0_row, product1)
             for h in (1, 0):
                 level1[h] = psum_part.tile([P, HALF1 // P, P], F32, name=f"level1_{h}", tag="part")
                 for which, term in enumerate(terms):
@@ -190,8 +193,6 @@ def tile_logictreeconv2d_kernel(tc, x, logits, offs, out):
             nc.scalar.copy(channels[:], level3[:])
             nc.sync.dma_start(out[r * P : (r + 1) * P, :], channels[:])
 
-        stages = ((pick_b, 0), (pick_a, 3), (turn_back, 1), (level_2, 5), (level_3, 6))
-        for step in range(POSITION_BLOCKS + max(lag for stage, lag in stages)):
-            for stage, lag in stages:
-                if 0 <= step - lag < POSITION_BLOCKS:
-                    stage(step - lag)
+        for stage in (pick_b, turn_back, rest_1, pick_a, level_2, level_3):
+            for r in range(POSITION_BLOCKS):
+                stage(r)

@@ -10,6 +10,8 @@ AXIS = mybir.AxisListType
 P = 128
 POSITIONS, ENTRIES = 512, 576
 POSITION_BLOCKS = POSITIONS // P
+PAIR = 2
+PAIRS = POSITION_BLOCKS // PAIR
 LIST = 1024
 LEVEL1 = LIST // 2
 LEVEL1_BLOCKS = LEVEL1 // P
@@ -24,8 +26,8 @@ def tile_logictreeconv2d_kernel(tc, x, logits, offs, out):
     with (
         tc.tile_pool(name="held", bufs=1) as held,
         tc.tile_pool(name="work", bufs=POSITION_BLOCKS) as work,
-        tc.psum_pool(name="psum_whole", bufs=1) as psum_whole,
-        tc.psum_pool(name="psum_part", bufs=6) as psum_part,
+        tc.psum_pool(name="psum_turns", bufs=2) as psum_turns,
+        tc.psum_pool(name="psum_level1", bufs=PAIRS) as psum_level1,
     ):
         kind_rows = held.tile([KINDS * GATE_BLOCKS, P], F32, name="kind_rows")
         nc.sync.dma_start(kind_rows[:], logits.rearrange("k (g n) -> (k g) n", n=P))
@@ -53,7 +55,7 @@ def tile_logictreeconv2d_kernel(tc, x, logits, offs, out):
         def spread(columns, name):
             row = held.tile([P, LEVEL1], F32, name=name)
             for h in range(LEVEL1 // HALF1):
-                piece = psum_part.tile([P, HALF1], F32, name="piece", tag="part")
+                piece = psum_turns.tile([P, HALF1], F32, name="piece", tag="turned")
                 for i in range(HALF1 // P):
                     g = h * (HALF1 // P) + i
                     nc.tensor.transpose(
@@ -64,7 +66,9 @@ def tile_logictreeconv2d_kernel(tc, x, logits, offs, out):
                 nc.scalar.copy(row[:, h * HALF1 : (h + 1) * HALF1], piece[:])
             return row
 
-        gate_kinds = psum_whole.tile([P, KINDS * GATE_BLOCKS], F32, name="gate_kinds", tag="turned")
+        gate_kinds = psum_turns.tile(
+            [P, KINDS * GATE_BLOCKS], F32, name="gate_kinds", tag="turned_back"
+        )
         nc.tensor.transpose(
             gate_kinds[:], kind_rows[:], identity[: KINDS * GATE_BLOCKS, : KINDS * GATE_BLOCKS]
         )
@@ -99,16 +103,21 @@ def tile_logictreeconv2d_kernel(tc, x, logits, offs, out):
         nc.vector.tensor_mul(weight[:], raw[:], inverse_sum[:].to_broadcast([P, 4, GATE_BLOCKS]))
 
         raw2_row = spread(raw[:, 2, :], "raw2_row")
-        weight0_row = spread(weight[:, 0, :], "weight0_row")
 
         def affine(dest, b, bias, scale):
             nc.scalar.activation(dest, b, ACT.Identity, bias=bias, scale=scale)
 
-        def bracket_of(dest, b, g):
-            affine(dest, b, bias=weight[:, 1, g : g + 1], scale=weight[:, 3, g : g + 1])
-
-        def rest_of(dest, b, g):
-            affine(dest, b, bias=weight[:, 0, g : g + 1], scale=weight[:, 2, g : g + 1])
+        below_a = weight[:, 0, 0:2]
+        below_b = weight[:, 0, 2:4]
+        level2_w = [weight[:, t, LEVEL2_BLOCK : LEVEL2_BLOCK + 2] for t in range(4)]
+        folded = held.tile([P, 3, 2], F32, name="folded")
+        partly = held.tile([P, 2], F32, name="partly")
+        for i in range(2):
+            one = slice(i, i + 1)
+            affine(folded[:, 1, one], below_b[:, one], bias=level2_w[1][:, one], scale=level2_w[3][:, one])
+            affine(folded[:, 2, one], below_a[:, one], bias=level2_w[2][:, one], scale=level2_w[3][:, one])
+            affine(partly[:, one], below_b[:, one], bias=level2_w[0][:, one], scale=level2_w[2][:, one])
+            affine(folded[:, 0, one], below_a[:, one], bias=partly[:, one], scale=folded[:, 1, one])
 
         kept = {}
 
@@ -117,7 +126,7 @@ def tile_logictreeconv2d_kernel(tc, x, logits, offs, out):
             nc.vector.tensor_tensor(
                 scaled_b[:], windows[r][:].indirect(list_b), inverse_row[:], ALU.mult
             )
-            turned = psum_whole.tile([P, LEVEL1_BLOCKS, P], F32, name="turned")
+            turned = psum_turns.tile([P, LEVEL1_BLOCKS, P], F32, name="turned")
             for g in range(LEVEL1_BLOCKS):
                 nc.tensor.transpose(turned[:, g, :], scaled_b[:, g * P : (g + 1) * P], identity[:])
             bracket_turned = work.tile([P, LEVEL1_BLOCKS, P], F32, name="bracket_turned")
@@ -131,7 +140,7 @@ def tile_logictreeconv2d_kernel(tc, x, logits, offs, out):
             kept["scaled_b", r], kept["bracket_turned", r] = scaled_b, bracket_turned
 
         def turn_back(r):
-            turned_back = psum_whole.tile([P, LEVEL1], F32, name="turned_back")
+            turned_back = psum_turns.tile([P, LEVEL1], F32, name="turned_back")
             for g in range(LEVEL1_BLOCKS):
                 nc.tensor.transpose(
                     turned_back[:, g * P : (g + 1) * P],
@@ -152,47 +161,80 @@ def tile_logictreeconv2d_kernel(tc, x, logits, offs, out):
             nc.vector.tensor_tensor(
                 product1[:], windows[r][:].indirect(list_a), kept["bracket1", r][:], ALU.mult
             )
-            level1 = {}
-            terms = (kept["rest1", r], weight0_row, product1)
+            q, j = divmod(r, PAIR)
+            if j == 0:
+                for h in range(2):
+                    kept["level1", h, q] = psum_level1.tile(
+                        [P, HALF1 // P, PAIR, P], F32, name=f"level1_{h}"
+                    )
+            terms = (kept["rest1", r], product1)
             for h in (1, 0):
-                level1[h] = psum_part.tile([P, HALF1 // P, P], F32, name=f"level1_{h}", tag="part")
                 for which, term in enumerate(terms):
                     for i in range(HALF1 // P):
                         g = h * (HALF1 // P) + i
                         add_turned(
-                            level1[h][:, i, :],
+                            kept["level1", h, q][:, i, j, :],
                             term[:, g * P : (g + 1) * P],
                             start=(which == 0 and i == 0),
                             stop=(which == len(terms) - 1 and i == HALF1 // P - 1),
                         )
-            bracket2 = work.tile([P, 2, P], F32, name="bracket2")
-            rest2 = work.tile([P, 2, P], F32, name="rest2")
-            for i in range(2):
-                bracket_of(bracket2[:, i, :], level1[1][:, i, :], LEVEL2_BLOCK + i)
-            for i in range(2):
-                rest_of(rest2[:, i, :], level1[1][:, i, :], LEVEL2_BLOCK + i)
-            kept["level1_a", r], kept["bracket2", r], kept["rest2", r] = level1[0], bracket2, rest2
 
-        def level_2(r):
-            level2 = work.tile([P, 2, P], F32, name="level2")
-            nc.vector.tensor_mul(level2[:], kept["level1_a", r][:], kept["bracket2", r][:])
-            nc.vector.tensor_add(level2[:], level2[:], kept["rest2", r][:])
-            bracket3 = work.tile([P, P], F32, name="bracket3")
-            rest3 = work.tile([P, P], F32, name="rest3")
-            bracket_of(bracket3[:], level2[:, 1, :], LEVEL3_BLOCK)
-            rest_of(rest3[:], level2[:, 1, :], LEVEL3_BLOCK)
-            kept["level2", r], kept["bracket3", r], kept["rest3", r] = level2, bracket3, rest3
+        def maps_2(q):
+            bracket2 = work.tile([P, 2, PAIR, P], F32, name="bracket2")
+            rest2 = work.tile([P, 2, PAIR, P], F32, name="rest2")
+            level1_b = kept["level1", 1, q]
+            for i in range(2):
+                affine(
+                    bracket2[:, i, :, :],
+                    level1_b[:, i, :, :],
+                    bias=folded[:, 1, i : i + 1],
+                    scale=level2_w[3][:, i : i + 1],
+                )
+            for i in range(2):
+                affine(
+                    rest2[:, i, :, :],
+                    level1_b[:, i, :, :],
+                    bias=folded[:, 0, i : i + 1],
+                    scale=folded[:, 2, i : i + 1],
+                )
+            kept["bracket2", q], kept["rest2", q] = bracket2, rest2
 
-        def level_3(r):
-            product3 = work.tile([P, P], F32, name="product3")
-            nc.vector.tensor_mul(product3[:], kept["level2", r][:, 0, :], kept["bracket3", r][:])
-            level3 = psum_part.tile([P, P], F32, name="level3", tag="part")
-            add_turned(level3[:], kept["rest3", r][:], start=True, stop=False)
-            add_turned(level3[:], product3[:], start=False, stop=True)
-            channels = work.tile([P, P], F32, name="channels")
+        def level_2(q):
+            level2 = work.tile([P, 2, PAIR, P], F32, name="level2")
+            nc.vector.tensor_mul(level2[:], kept["level1", 0, q][:], kept["bracket2", q][:])
+            nc.vector.tensor_add(level2[:], level2[:], kept["rest2", q][:])
+            bracket3 = work.tile([P, PAIR, P], F32, name="bracket3")
+            rest3 = work.tile([P, PAIR, P], F32, name="rest3")
+            level3_w = [weight[:, t, LEVEL3_BLOCK : LEVEL3_BLOCK + 1] for t in range(4)]
+            affine(bracket3[:], level2[:, 1, :, :], bias=level3_w[1], scale=level3_w[3])
+            affine(rest3[:], level2[:, 1, :, :], bias=level3_w[0], scale=level3_w[2])
+            kept["level2", q], kept["bracket3", q], kept["rest3", q] = level2, bracket3, rest3
+
+        def level_3(q):
+            product3 = work.tile([P, PAIR, P], F32, name="product3")
+            nc.vector.tensor_mul(product3[:], kept["level2", q][:, 0, :, :], kept["bracket3", q][:])
+            level3 = psum_turns.tile([P, PAIR, P], F32, name="level3", tag="turned_back")
+            terms = (kept["rest3", q], product3)
+            for which, term in enumerate(terms):
+                for j in range(PAIR):
+                    add_turned(
+                        level3[:, j, :],
+                        term[:, j, :],
+                        start=(which == 0 and j == 0),
+                        stop=(which == len(terms) - 1 and j == PAIR - 1),
+                    )
+            channels = work.tile([P, PAIR, P], F32, name="channels")
             nc.scalar.copy(channels[:], level3[:])
-            nc.sync.dma_start(out[r * P : (r + 1) * P, :], channels[:])
+            rows = out[q * PAIR * P : (q + 1) * PAIR * P, :]
+            nc.sync.dma_start(rows.rearrange("(j p) c -> p j c", p=P), channels[:])
 
-        for stage in (pick_b, turn_back, rest_1, pick_a, level_2, level_3):
+        for stage in (pick_b, turn_back, rest_1):
             for r in range(POSITION_BLOCKS):
                 stage(r)
+        for q in range(PAIRS):
+            for j in range(PAIR):
+                pick_a(q * PAIR + j)
+            maps_2(q)
+        for stage in (level_2, level_3):
+            for q in range(PAIRS):
+                stage(q)

@@ -119,6 +119,12 @@ def tile_logictreeconv2d_kernel(tc, x, logits, offs, out):
             affine(partly[:, one], below_b[:, one], bias=level2_w[0][:, one], scale=level2_w[2][:, one])
             affine(folded[:, 0, one], below_a[:, one], bias=partly[:, one], scale=folded[:, 1, one])
 
+        level3_w = [weight[:, t, LEVEL3_BLOCK : LEVEL3_BLOCK + 1] for t in range(4)]
+        early = held.tile([P, 2, 2], F32, name="early")
+        for which, (t_bias, t_scale) in enumerate(((1, 3), (0, 2))):
+            affine(early[:, which, 0:1], folded[:, 0, 1:2], bias=level3_w[t_bias], scale=level3_w[t_scale])
+            affine(early[:, which, 1:2], folded[:, 2, 1:2], bias=0.0, scale=level3_w[t_scale])
+
         kept = {}
 
         def pick_b(r):
@@ -180,9 +186,8 @@ def tile_logictreeconv2d_kernel(tc, x, logits, offs, out):
                         )
 
         def maps_2(q):
-            bracket2 = work.tile([P, 2, PAIR, P], F32, name="bracket2")
-            rest2 = work.tile([P, 2, PAIR, P], F32, name="rest2")
             level1_b = kept["level1", 1, q]
+            bracket2 = work.tile([P, 2, PAIR, P], F32, name="bracket2")
             for i in range(2):
                 affine(
                     bracket2[:, i, :, :],
@@ -190,31 +195,33 @@ def tile_logictreeconv2d_kernel(tc, x, logits, offs, out):
                     bias=folded[:, 1, i : i + 1],
                     scale=level2_w[3][:, i : i + 1],
                 )
-            for i in range(2):
-                affine(
-                    rest2[:, i, :, :],
-                    level1_b[:, i, :, :],
-                    bias=folded[:, 0, i : i + 1],
-                    scale=folded[:, 2, i : i + 1],
-                )
-            kept["bracket2", q], kept["rest2", q] = bracket2, rest2
+            early3 = work.tile([P, 2, PAIR, P], F32, name="early3")
+            rest2 = work.tile([P, PAIR, P], F32, name="rest2")
+            affine(early3[:, 0, :, :], level1_b[:, 1, :, :], bias=early[:, 0, 0:1], scale=early[:, 0, 1:2])
+            affine(rest2[:], level1_b[:, 0, :, :], bias=folded[:, 0, 0:1], scale=folded[:, 2, 0:1])
+            affine(early3[:, 1, :, :], level1_b[:, 1, :, :], bias=early[:, 1, 0:1], scale=early[:, 1, 1:2])
+            kept["bracket2", q], kept["early3", q], kept["rest2", q] = bracket2, early3, rest2
 
-        def level_2(q):
-            level2 = work.tile([P, 2, PAIR, P], F32, name="level2")
-            nc.vector.tensor_mul(level2[:], kept["level1", 0, q][:], kept["bracket2", q][:])
-            nc.vector.tensor_add(level2[:], level2[:], kept["rest2", q][:])
+        def levels_2_3(q):
+            product2 = work.tile([P, 2, PAIR, P], F32, name="product2")
+            nc.vector.tensor_mul(product2[:], kept["level1", 0, q][:], kept["bracket2", q][:])
             bracket3 = work.tile([P, PAIR, P], F32, name="bracket3")
-            rest3 = work.tile([P, PAIR, P], F32, name="rest3")
-            level3_w = [weight[:, t, LEVEL3_BLOCK : LEVEL3_BLOCK + 1] for t in range(4)]
-            affine(bracket3[:], level2[:, 1, :, :], bias=level3_w[1], scale=level3_w[3])
-            affine(rest3[:], level2[:, 1, :, :], bias=level3_w[0], scale=level3_w[2])
-            kept["level2", q], kept["bracket3", q], kept["rest3", q] = level2, bracket3, rest3
-
-        def level_3(q):
+            nc.vector.scalar_tensor_tensor(
+                bracket3[:],
+                product2[:, 1, :, :],
+                level3_w[3],
+                kept["early3", q][:, 0, :, :],
+                op0=ALU.mult,
+                op1=ALU.add,
+            )
+            late3 = work.tile([P, PAIR, P], F32, name="late3")
+            affine(late3[:], product2[:, 1, :, :], bias=0.0, scale=level3_w[2])
+            level2_a = work.tile([P, PAIR, P], F32, name="level2_a")
+            nc.vector.tensor_add(level2_a[:], product2[:, 0, :, :], kept["rest2", q][:])
             product3 = work.tile([P, PAIR, P], F32, name="product3")
-            nc.vector.tensor_mul(product3[:], kept["level2", q][:, 0, :, :], kept["bracket3", q][:])
+            nc.vector.tensor_mul(product3[:], level2_a[:], bracket3[:])
             level3 = psum_turns.tile([P, PAIR, P], F32, name="level3", tag="turned_back")
-            terms = (kept["rest3", q], product3)
+            terms = (kept["early3", q][:, 1, :, :], late3[:], product3[:])
             for which, term in enumerate(terms):
                 for j in range(PAIR):
                     add_turned(
@@ -235,6 +242,5 @@ def tile_logictreeconv2d_kernel(tc, x, logits, offs, out):
             for j in range(PAIR):
                 pick_a(q * PAIR + j)
             maps_2(q)
-        for stage in (level_2, level_3):
-            for q in range(PAIRS):
-                stage(q)
+        for q in range(PAIRS):
+            levels_2_3(q)

@@ -17,6 +17,7 @@ LEVEL1 = LIST // 2
 LEVEL1_BLOCKS = LEVEL1 // P
 HALF1 = LEVEL1 // 2
 KINDS = 16
+LOAD_ROWS = 64
 GATE_BLOCKS = 7
 LEVEL2_BLOCK, LEVEL3_BLOCK = 4, 6
 
@@ -29,8 +30,11 @@ def tile_logictreeconv2d_kernel(tc, x, logits, offs, out):
         tc.psum_pool(name="psum_turns", bufs=2) as psum_turns,
         tc.psum_pool(name="psum_level1", bufs=PAIRS) as psum_level1,
     ):
-        kind_rows = held.tile([KINDS * GATE_BLOCKS, P], F32, name="kind_rows")
-        nc.sync.dma_start(kind_rows[:], logits.rearrange("k (g n) -> (k g) n", n=P))
+        rows = logits.rearrange("k (g n) -> (k g) n", n=P)
+        first_rows = (0, KINDS * GATE_BLOCKS - LOAD_ROWS)
+        kind_rows = [held.tile([LOAD_ROWS, P], F32, name=f"kind_rows{n}") for n in range(2)]
+        for n, queue in enumerate((nc.sync, nc.scalar)):
+            queue.dma_start(kind_rows[n][:], rows[first_rows[n] : first_rows[n] + LOAD_ROWS, :])
 
         offsets = held.tile([P, LIST // 16], U16, name="offsets")
         nc.sync.dma_start(offsets[:], offs)
@@ -69,9 +73,12 @@ def tile_logictreeconv2d_kernel(tc, x, logits, offs, out):
         gate_kinds = psum_turns.tile(
             [P, KINDS * GATE_BLOCKS], F32, name="gate_kinds", tag="turned_back"
         )
-        nc.tensor.transpose(
-            gate_kinds[:], kind_rows[:], identity[: KINDS * GATE_BLOCKS, : KINDS * GATE_BLOCKS]
-        )
+        for n in range(2):
+            nc.tensor.transpose(
+                gate_kinds[:, first_rows[n] : first_rows[n] + LOAD_ROWS],
+                kind_rows[n][:],
+                identity[:LOAD_ROWS, :LOAD_ROWS],
+            )
         by_kind = gate_kinds[:].rearrange("p (k g) -> p k g", g=GATE_BLOCKS)
 
         largest = held.tile([P, GATE_BLOCKS], F32, name="largest")

@@ -10,8 +10,8 @@ AXIS = mybir.AxisListType
 P = 128
 POSITIONS, ENTRIES = 512, 576
 POSITION_BLOCKS = POSITIONS // P
-PAIR = 2
-PAIRS = POSITION_BLOCKS // PAIR
+UNITS = ((0, 1), (2,), (3,))
+LEVEL1_BANKS = 2
 LIST = 1024
 LEVEL1 = LIST // 2
 LEVEL1_BLOCKS = LEVEL1 // P
@@ -28,7 +28,7 @@ def tile_logictreeconv2d_kernel(tc, x, logits, offs, out):
         tc.tile_pool(name="held", bufs=1) as held,
         tc.tile_pool(name="work", bufs=POSITION_BLOCKS) as work,
         tc.psum_pool(name="psum_turns", bufs=2) as psum_turns,
-        tc.psum_pool(name="psum_level1", bufs=PAIRS) as psum_level1,
+        tc.psum_pool(name="psum_level1", bufs=LEVEL1_BANKS) as psum_level1,
     ):
         rows = logits.rearrange("k (g n) -> (k g) n", n=P)
         first_rows = (0, KINDS * GATE_BLOCKS - LOAD_ROWS)
@@ -81,24 +81,29 @@ def tile_logictreeconv2d_kernel(tc, x, logits, offs, out):
             )
         by_kind = gate_kinds[:].rearrange("p (k g) -> p k g", g=GATE_BLOCKS)
 
-        largest = held.tile([P, GATE_BLOCKS], F32, name="largest")
-        nc.vector.reduce_max(largest[:], by_kind.rearrange("p k g -> p g k"), axis=AXIS.X)
-        exps = held.tile([P, KINDS, GATE_BLOCKS], F32, name="exps")
-        nc.vector.tensor_sub(
-            exps[:], by_kind, largest[:].unsqueeze(1).to_broadcast([P, KINDS, GATE_BLOCKS])
+        minus_largest = held.tile([P, GATE_BLOCKS], F32, name="minus_largest")
+        nc.vector.reduce_max(
+            minus_largest[:], by_kind.rearrange("p k g -> p g k"), axis=AXIS.X, negate=True
         )
-        nc.scalar.activation(exps[:], exps[:], ACT.Exp)
+        exps = held.tile([P, GATE_BLOCKS, KINDS], F32, name="exps")
+        sums = held.tile([P, GATE_BLOCKS], F32, name="sums")
+        for g in range(GATE_BLOCKS):
+            nc.scalar.activation(
+                exps[:, g, :],
+                by_kind[:, :, g],
+                ACT.Exp,
+                bias=minus_largest[:, g : g + 1],
+                accum_out=sums[:, g : g + 1],
+            )
         inverse_sum = held.tile([P, 1, GATE_BLOCKS], F32, name="inverse_sum")
-        nc.vector.reduce_sum(
-            inverse_sum[:, 0, :], exps[:].rearrange("p k g -> p g k"), axis=AXIS.X
-        )
-        nc.vector.reciprocal(inverse_sum[:], inverse_sum[:])
+        for level in (slice(0, LEVEL1_BLOCKS), slice(LEVEL1_BLOCKS, GATE_BLOCKS)):
+            nc.vector.reciprocal(inverse_sum[:, 0, level], sums[:, level])
 
         inverse_row = spread(inverse_sum[:, 0, :], "inverse_row")
 
         raw = held.tile([P, 4, GATE_BLOCKS], F32, name="raw")
         for place, bit in enumerate((3, 1, 2, 0)):
-            with_bit = exps[:].rearrange("p (hi two lo) g -> p two g hi lo", two=2, lo=2**bit)
+            with_bit = exps[:].rearrange("p g (hi two lo) -> p two g hi lo", two=2, lo=2**bit)
             nc.vector.reduce_sum(raw[:, place, :], with_bit[:, 1], axis=AXIS.XY)
 
         nc.vector.tensor_sub(raw[:, 3, :], raw[:, 3, :], raw[:, 1, :])
@@ -169,32 +174,36 @@ def tile_logictreeconv2d_kernel(tc, x, logits, offs, out):
             nc.vector.tensor_mul(rest1[:], kept["scaled_b", r][:], raw2_row[:])
             kept["rest1", r] = rest1
 
-        def pick_a(r):
+        def pick_a(u, j):
+            r, n = UNITS[u][j], len(UNITS[u])
             product1 = work.tile([P, LEVEL1], F32, name="product1")
             nc.vector.tensor_tensor(
                 product1[:], windows[r][:].indirect(list_a), kept["bracket1", r][:], ALU.mult
             )
-            q, j = divmod(r, PAIR)
             if j == 0:
                 for h in range(2):
-                    kept["level1", h, q] = psum_level1.tile(
-                        [P, HALF1 // P, PAIR, P], F32, name=f"level1_{h}"
-                    )
+                    shape = [P, HALF1 // P, n, P]
+                    if u < LEVEL1_BANKS:
+                        sums1 = psum_level1.tile(shape, F32, name=f"level1_{h}")
+                    else:
+                        sums1 = psum_turns.tile(shape, F32, name="level1", tag="turned")
+                    kept["level1", h, u] = sums1
             terms = (kept["rest1", r], product1)
             for h in (1, 0):
                 for which, term in enumerate(terms):
                     for i in range(HALF1 // P):
                         g = h * (HALF1 // P) + i
                         add_turned(
-                            kept["level1", h, q][:, i, j, :],
+                            kept["level1", h, u][:, i, j, :],
                             term[:, g * P : (g + 1) * P],
                             start=(which == 0 and i == 0),
                             stop=(which == len(terms) - 1 and i == HALF1 // P - 1),
                         )
 
-        def maps_2(q):
-            level1_b = kept["level1", 1, q]
-            bracket2 = work.tile([P, 2, PAIR, P], F32, name="bracket2")
+        def maps_2(u):
+            n = len(UNITS[u])
+            level1_b = kept["level1", 1, u]
+            bracket2 = work.tile([P, 2, n, P], F32, name=f"bracket2_{n}")
             for i in range(2):
                 affine(
                     bracket2[:, i, :, :],
@@ -202,52 +211,63 @@ def tile_logictreeconv2d_kernel(tc, x, logits, offs, out):
                     bias=folded[:, 1, i : i + 1],
                     scale=level2_w[3][:, i : i + 1],
                 )
-            early3 = work.tile([P, 2, PAIR, P], F32, name="early3")
-            rest2 = work.tile([P, PAIR, P], F32, name="rest2")
+            early3 = work.tile([P, 2, n, P], F32, name=f"early3_{n}")
+            rest2 = work.tile([P, n, P], F32, name=f"rest2_{n}")
             affine(early3[:, 0, :, :], level1_b[:, 1, :, :], bias=early[:, 0, 0:1], scale=early[:, 0, 1:2])
             affine(rest2[:], level1_b[:, 0, :, :], bias=folded[:, 0, 0:1], scale=folded[:, 2, 0:1])
             affine(early3[:, 1, :, :], level1_b[:, 1, :, :], bias=early[:, 1, 0:1], scale=early[:, 1, 1:2])
-            kept["bracket2", q], kept["early3", q], kept["rest2", q] = bracket2, early3, rest2
+            kept["bracket2", u], kept["early3", u], kept["rest2", u] = bracket2, early3, rest2
 
-        def levels_2_3(q):
-            product2 = work.tile([P, 2, PAIR, P], F32, name="product2")
-            nc.vector.tensor_mul(product2[:], kept["level1", 0, q][:], kept["bracket2", q][:])
-            bracket3 = work.tile([P, PAIR, P], F32, name="bracket3")
+        def products_2(u):
+            product2 = work.tile([P, 2, len(UNITS[u]), P], F32, name=f"product2_{len(UNITS[u])}")
+            nc.vector.tensor_mul(product2[:], kept["level1", 0, u][:], kept["bracket2", u][:])
+            kept["product2", u] = product2
+
+        def factors_3(u):
+            n = len(UNITS[u])
+            product2 = kept["product2", u]
+            bracket3 = work.tile([P, n, P], F32, name=f"bracket3_{n}")
             nc.vector.scalar_tensor_tensor(
                 bracket3[:],
                 product2[:, 1, :, :],
                 level3_w[3],
-                kept["early3", q][:, 0, :, :],
+                kept["early3", u][:, 0, :, :],
                 op0=ALU.mult,
                 op1=ALU.add,
             )
-            late3 = work.tile([P, PAIR, P], F32, name="late3")
+            late3 = work.tile([P, n, P], F32, name=f"late3_{n}")
             affine(late3[:], product2[:, 1, :, :], bias=0.0, scale=level3_w[2])
-            level2_a = work.tile([P, PAIR, P], F32, name="level2_a")
-            nc.vector.tensor_add(level2_a[:], product2[:, 0, :, :], kept["rest2", q][:])
-            product3 = work.tile([P, PAIR, P], F32, name="product3")
-            nc.vector.tensor_mul(product3[:], level2_a[:], bracket3[:])
-            level3 = psum_turns.tile([P, PAIR, P], F32, name="level3", tag="turned_back")
-            terms = (kept["early3", q][:, 1, :, :], late3[:], product3[:])
+            level2_a = work.tile([P, n, P], F32, name=f"level2_a_{n}")
+            nc.vector.tensor_add(level2_a[:], product2[:, 0, :, :], kept["rest2", u][:])
+            kept["bracket3", u], kept["late3", u], kept["level2_a", u] = bracket3, late3, level2_a
+
+        def level_3(u):
+            n = len(UNITS[u])
+            product3 = work.tile([P, n, P], F32, name=f"product3_{n}")
+            nc.vector.tensor_mul(product3[:], kept["level2_a", u][:], kept["bracket3", u][:])
+            level3 = psum_turns.tile([P, n, P], F32, name="level3", tag="turned_back")
+            terms = (kept["early3", u][:, 1, :, :], kept["late3", u][:], product3[:])
             for which, term in enumerate(terms):
-                for j in range(PAIR):
+                for j in range(n):
                     add_turned(
                         level3[:, j, :],
                         term[:, j, :],
                         start=(which == 0 and j == 0),
-                        stop=(which == len(terms) - 1 and j == PAIR - 1),
+                        stop=(which == len(terms) - 1 and j == n - 1),
                     )
-            channels = work.tile([P, PAIR, P], F32, name="channels")
+            channels = work.tile([P, n, P], F32, name=f"channels_{n}")
             nc.scalar.copy(channels[:], level3[:])
-            rows = out[q * PAIR * P : (q + 1) * PAIR * P, :]
+            first = UNITS[u][0]
+            rows = out[first * P : (first + n) * P, :]
             nc.sync.dma_start(rows.rearrange("(j p) c -> p j c", p=P), channels[:])
 
         for stage in (pick_b, turn_back, rest_1):
             for r in range(POSITION_BLOCKS):
                 stage(r)
-        for q in range(PAIRS):
-            for j in range(PAIR):
-                pick_a(q * PAIR + j)
-            maps_2(q)
-        for q in range(PAIRS):
-            levels_2_3(q)
+        for u in range(len(UNITS)):
+            for j in range(len(UNITS[u])):
+                pick_a(u, j)
+            maps_2(u)
+        for stage in (products_2, factors_3, level_3):
+            for u in range(len(UNITS)):
+                stage(u)

@@ -11,7 +11,8 @@ P = 128
 POSITIONS, ENTRIES = 512, 576
 POSITION_BLOCKS = POSITIONS // P
 UNITS = ((0, 1), (2,), (3,))
-LEVEL1_BANKS = 2
+PSUM_BANKS = 8
+TENSOR_RESTS = 2
 LIST = 1024
 LEVEL1 = LIST // 2
 LEVEL1_BLOCKS = LEVEL1 // P
@@ -27,8 +28,7 @@ def tile_logictreeconv2d_kernel(tc, x, logits, offs, out):
     with (
         tc.tile_pool(name="held", bufs=1) as held,
         tc.tile_pool(name="work", bufs=POSITION_BLOCKS) as work,
-        tc.psum_pool(name="psum_turns", bufs=2) as psum_turns,
-        tc.psum_pool(name="psum_level1", bufs=LEVEL1_BANKS) as psum_level1,
+        tc.psum_pool(name="psum", bufs=PSUM_BANKS) as psum,
     ):
         rows = logits.rearrange("k (g n) -> (k g) n", n=P)
         first_rows = (0, KINDS * GATE_BLOCKS - LOAD_ROWS)
@@ -59,7 +59,7 @@ def tile_logictreeconv2d_kernel(tc, x, logits, offs, out):
         def spread(columns, name):
             row = held.tile([P, LEVEL1], F32, name=name)
             for h in range(LEVEL1 // HALF1):
-                piece = psum_turns.tile([P, HALF1], F32, name="piece", tag="turned")
+                piece = psum.tile([P, HALF1], F32, name="piece", tag="bank")
                 for i in range(HALF1 // P):
                     g = h * (HALF1 // P) + i
                     nc.tensor.transpose(
@@ -70,9 +70,7 @@ def tile_logictreeconv2d_kernel(tc, x, logits, offs, out):
                 nc.scalar.copy(row[:, h * HALF1 : (h + 1) * HALF1], piece[:])
             return row
 
-        gate_kinds = psum_turns.tile(
-            [P, KINDS * GATE_BLOCKS], F32, name="gate_kinds", tag="turned_back"
-        )
+        gate_kinds = psum.tile([P, KINDS * GATE_BLOCKS], F32, name="gate_kinds", tag="bank")
         for n in range(2):
             nc.tensor.transpose(
                 gate_kinds[:, first_rows[n] : first_rows[n] + LOAD_ROWS],
@@ -116,6 +114,12 @@ def tile_logictreeconv2d_kernel(tc, x, logits, offs, out):
 
         raw2_row = spread(raw[:, 2, :], "raw2_row")
 
+        diagonals = held.tile([P, LEVEL1_BLOCKS, P], F32, name="diagonals")
+        for g in range(LEVEL1_BLOCKS):
+            nc.scalar.activation(
+                diagonals[:, g, :], identity[:], ACT.Copy, scale=raw[:, 2, g : g + 1]
+            )
+
         def affine(dest, b, bias, scale):
             nc.scalar.activation(dest, b, ACT.Identity, bias=bias, scale=scale)
 
@@ -144,7 +148,7 @@ def tile_logictreeconv2d_kernel(tc, x, logits, offs, out):
             nc.vector.tensor_tensor(
                 scaled_b[:], windows[r][:].indirect(list_b), inverse_row[:], ALU.mult
             )
-            turned = psum_turns.tile([P, LEVEL1_BLOCKS, P], F32, name="turned")
+            turned = psum.tile([P, LEVEL1_BLOCKS, P], F32, name="turned", tag="bank")
             for g in range(LEVEL1_BLOCKS):
                 nc.tensor.transpose(turned[:, g, :], scaled_b[:, g * P : (g + 1) * P], identity[:])
             bracket_turned = work.tile([P, LEVEL1_BLOCKS, P], F32, name="bracket_turned")
@@ -155,10 +159,11 @@ def tile_logictreeconv2d_kernel(tc, x, logits, offs, out):
                     bias=weight[:, 1, g : g + 1],
                     scale=raw[:, 3, g : g + 1],
                 )
-            kept["scaled_b", r], kept["bracket_turned", r] = scaled_b, bracket_turned
+            kept["scaled_b", r], kept["turned", r] = scaled_b, turned
+            kept["bracket_turned", r] = bracket_turned
 
         def turn_back(r):
-            turned_back = psum_turns.tile([P, LEVEL1], F32, name="turned_back")
+            turned_back = psum.tile([P, LEVEL1], F32, name="turned_back", tag="bank")
             for g in range(LEVEL1_BLOCKS):
                 nc.tensor.transpose(
                     turned_back[:, g * P : (g + 1) * P],
@@ -170,9 +175,37 @@ def tile_logictreeconv2d_kernel(tc, x, logits, offs, out):
             kept["bracket1", r] = bracket1
 
         def rest_1(r):
-            rest1 = work.tile([P, LEVEL1], F32, name="rest1")
-            nc.vector.tensor_mul(rest1[:], kept["scaled_b", r][:], raw2_row[:])
-            kept["rest1", r] = rest1
+            if r < TENSOR_RESTS:
+                b_turned = work.tile([P, LEVEL1_BLOCKS, P], F32, name="b_turned")
+                nc.scalar.copy(b_turned[:], kept["turned", r][:])
+                kept["b_turned", r] = b_turned
+            else:
+                rest1 = work.tile([P, LEVEL1], F32, name="rest1")
+                nc.vector.tensor_mul(rest1[:], kept["scaled_b", r][:], raw2_row[:])
+                kept["rest1", r] = rest1
+
+        def sum_rest(u, j):
+            r, n = UNITS[u][j], len(UNITS[u])
+            for h in (1, 0):
+                if j == 0:
+                    kept["level1", h, u] = psum.tile(
+                        [P, HALF1 // P, n, P], F32, name="level1", tag="bank"
+                    )
+                for i in range(HALF1 // P):
+                    g = h * (HALF1 // P) + i
+                    part = kept["level1", h, u][:, i, j, :]
+                    start = i == 0 and j == 0
+                    if r < TENSOR_RESTS:
+                        nc.tensor.matmul(
+                            part,
+                            diagonals[:, g, :],
+                            kept["b_turned", r][:, g, :],
+                            start=start,
+                            stop=False,
+                        )
+                    else:
+                        rest = kept["rest1", r][:, g * P : (g + 1) * P]
+                        add_turned(part, rest, start=start, stop=False)
 
         def pick_a(u, j):
             r, n = UNITS[u][j], len(UNITS[u])
@@ -180,25 +213,15 @@ def tile_logictreeconv2d_kernel(tc, x, logits, offs, out):
             nc.vector.tensor_tensor(
                 product1[:], windows[r][:].indirect(list_a), kept["bracket1", r][:], ALU.mult
             )
-            if j == 0:
-                for h in range(2):
-                    shape = [P, HALF1 // P, n, P]
-                    if u < LEVEL1_BANKS:
-                        sums1 = psum_level1.tile(shape, F32, name=f"level1_{h}")
-                    else:
-                        sums1 = psum_turns.tile(shape, F32, name="level1", tag="turned")
-                    kept["level1", h, u] = sums1
-            terms = (kept["rest1", r], product1)
             for h in (1, 0):
-                for which, term in enumerate(terms):
-                    for i in range(HALF1 // P):
-                        g = h * (HALF1 // P) + i
-                        add_turned(
-                            kept["level1", h, u][:, i, j, :],
-                            term[:, g * P : (g + 1) * P],
-                            start=(which == 0 and i == 0),
-                            stop=(which == len(terms) - 1 and i == HALF1 // P - 1),
-                        )
+                for i in range(HALF1 // P):
+                    g = h * (HALF1 // P) + i
+                    add_turned(
+                        kept["level1", h, u][:, i, j, :],
+                        product1[:, g * P : (g + 1) * P],
+                        start=False,
+                        stop=(i == HALF1 // P - 1 and j == n - 1),
+                    )
 
         def maps_2(u):
             n = len(UNITS[u])
@@ -245,7 +268,7 @@ def tile_logictreeconv2d_kernel(tc, x, logits, offs, out):
             n = len(UNITS[u])
             product3 = work.tile([P, n, P], F32, name=f"product3_{n}")
             nc.vector.tensor_mul(product3[:], kept["level2_a", u][:], kept["bracket3", u][:])
-            level3 = psum_turns.tile([P, n, P], F32, name="level3", tag="turned_back")
+            level3 = psum.tile([P, n, P], F32, name="level3", tag="bank")
             terms = (kept["early3", u][:, 1, :, :], kept["late3", u][:], product3[:])
             for which, term in enumerate(terms):
                 for j in range(n):
@@ -261,13 +284,19 @@ def tile_logictreeconv2d_kernel(tc, x, logits, offs, out):
             rows = out[first * P : (first + n) * P, :]
             nc.sync.dma_start(rows.rearrange("(j p) c -> p j c", p=P), channels[:])
 
-        for stage in (pick_b, turn_back, rest_1):
-            for r in range(POSITION_BLOCKS):
-                stage(r)
-        for u in range(len(UNITS)):
-            for j in range(len(UNITS[u])):
+        places = [(u, j) for u in range(len(UNITS)) for j in range(len(UNITS[u]))]
+        for step in range(POSITION_BLOCKS + 3):
+            if step < POSITION_BLOCKS:
+                pick_b(step)
+            if 1 <= step <= POSITION_BLOCKS:
+                turn_back(step - 1)
+                rest_1(step - 1)
+            if 3 <= step:
+                u, j = places[step - 3]
+                sum_rest(u, j)
                 pick_a(u, j)
-            maps_2(u)
+                if j == len(UNITS[u]) - 1:
+                    maps_2(u)
         for stage in (products_2, factors_3, level_3):
             for u in range(len(UNITS)):
                 stage(u)

@@ -17,6 +17,7 @@ LIST = 1024
 LEVEL1 = LIST // 2
 LEVEL1_BLOCKS = LEVEL1 // P
 HALF1 = LEVEL1 // 2
+PIECES = ((0, P), (P, HALF1), (HALF1, LEVEL1))
 KINDS = 16
 LOAD_ROWS = 64
 GATE_BLOCKS = 7
@@ -58,16 +59,15 @@ def tile_logictreeconv2d_kernel(tc, x, logits, offs, out):
 
         def spread(columns, name):
             row = held.tile([P, LEVEL1], F32, name=name)
-            for h in range(LEVEL1 // HALF1):
-                piece = psum.tile([P, HALF1], F32, name="piece", tag="bank")
-                for i in range(HALF1 // P):
-                    g = h * (HALF1 // P) + i
+            for lo, hi in PIECES:
+                piece = psum.tile([P, hi - lo], F32, name="piece", tag="bank")
+                for n in range(lo, hi, P):
                     nc.tensor.transpose(
-                        piece[:, i * P : (i + 1) * P],
-                        columns[:, g : g + 1].to_broadcast([P, P]),
+                        piece[:, n - lo : n - lo + P],
+                        columns[:, n // P : n // P + 1].to_broadcast([P, P]),
                         identity[:],
                     )
-                nc.scalar.copy(row[:, h * HALF1 : (h + 1) * HALF1], piece[:])
+                nc.scalar.copy(row[:, lo:hi], piece[:])
             return row
 
         gate_kinds = psum.tile([P, KINDS * GATE_BLOCKS], F32, name="gate_kinds", tag="bank")
@@ -94,8 +94,9 @@ def tile_logictreeconv2d_kernel(tc, x, logits, offs, out):
                 accum_out=sums[:, g : g + 1],
             )
         inverse_sum = held.tile([P, 1, GATE_BLOCKS], F32, name="inverse_sum")
-        for level in (slice(0, LEVEL1_BLOCKS), slice(LEVEL1_BLOCKS, GATE_BLOCKS)):
-            nc.vector.reciprocal(inverse_sum[:, 0, level], sums[:, level])
+        for lo, hi in (*PIECES, (LEVEL1, GATE_BLOCKS * P)):
+            blocks = slice(lo // P, hi // P)
+            nc.vector.reciprocal(inverse_sum[:, 0, blocks], sums[:, blocks])
 
         inverse_row = spread(inverse_sum[:, 0, :], "inverse_row")
 
@@ -145,9 +146,13 @@ def tile_logictreeconv2d_kernel(tc, x, logits, offs, out):
 
         def pick_b(r):
             scaled_b = work.tile([P, LEVEL1], F32, name="scaled_b")
-            nc.vector.tensor_tensor(
-                scaled_b[:], windows[r][:].indirect(list_b), inverse_row[:], ALU.mult
-            )
+            for lo, hi in PIECES if r == 0 else ((0, LEVEL1),):
+                nc.vector.tensor_tensor(
+                    scaled_b[:, lo:hi],
+                    windows[r][:].indirect(list_b[:, lo // 16 : hi // 16]),
+                    inverse_row[:, lo:hi],
+                    ALU.mult,
+                )
             turned = psum.tile([P, LEVEL1_BLOCKS, P], F32, name="turned", tag="bank")
             for g in range(LEVEL1_BLOCKS):
                 nc.tensor.transpose(turned[:, g, :], scaled_b[:, g * P : (g + 1) * P], identity[:])
@@ -243,7 +248,13 @@ def tile_logictreeconv2d_kernel(tc, x, logits, offs, out):
 
         def products_2(u):
             product2 = work.tile([P, 2, len(UNITS[u]), P], F32, name=f"product2_{len(UNITS[u])}")
-            nc.vector.tensor_mul(product2[:], kept["level1", 0, u][:], kept["bracket2", u][:])
+            last = u == len(UNITS) - 1
+            for blocks in (slice(1, 2), slice(0, 1)) if last else (slice(0, 2),):
+                nc.vector.tensor_mul(
+                    product2[:, blocks],
+                    kept["level1", 0, u][:, blocks],
+                    kept["bracket2", u][:, blocks],
+                )
             kept["product2", u] = product2
 
         def factors_3(u):

@@ -120,6 +120,10 @@ def tile_logictreeconv2d_kernel(tc, x, logits, offs, out):
             nc.scalar.activation(
                 diagonals[:, g, :], identity[:], ACT.Copy, scale=raw[:, 2, g : g + 1]
             )
+        diagonal3 = held.tile([P, P], F32, name="diagonal3")
+        nc.scalar.activation(
+            diagonal3[:], identity[:], ACT.Copy, scale=weight[:, 2, LEVEL3_BLOCK : LEVEL3_BLOCK + 1]
+        )
 
         def affine(dest, b, bias, scale):
             nc.scalar.activation(dest, b, ACT.Identity, bias=bias, scale=scale)
@@ -269,26 +273,28 @@ def tile_logictreeconv2d_kernel(tc, x, logits, offs, out):
                 op0=ALU.mult,
                 op1=ALU.add,
             )
-            late3 = work.tile([P, n, P], F32, name=f"late3_{n}")
-            affine(late3[:], product2[:, 1, :, :], bias=0.0, scale=level3_w[2])
             level2_a = work.tile([P, n, P], F32, name=f"level2_a_{n}")
             nc.vector.tensor_add(level2_a[:], product2[:, 0, :, :], kept["rest2", u][:])
-            kept["bracket3", u], kept["late3", u], kept["level2_a", u] = bracket3, late3, level2_a
+            kept["bracket3", u], kept["level2_a", u] = bracket3, level2_a
 
         def level_3(u):
             n = len(UNITS[u])
             product3 = work.tile([P, n, P], F32, name=f"product3_{n}")
             nc.vector.tensor_mul(product3[:], kept["level2_a", u][:], kept["bracket3", u][:])
             level3 = psum.tile([P, n, P], F32, name="level3", tag="bank")
-            terms = (kept["early3", u][:, 1, :, :], kept["late3", u][:], product3[:])
-            for which, term in enumerate(terms):
-                for j in range(n):
-                    add_turned(
-                        level3[:, j, :],
-                        term[:, j, :],
-                        start=(which == 0 and j == 0),
-                        stop=(which == len(terms) - 1 and j == n - 1),
-                    )
+            for j in range(n):
+                early_rest = kept["early3", u][:, 1, j, :]
+                add_turned(level3[:, j, :], early_rest, start=(j == 0), stop=False)
+            for j in range(n):
+                nc.tensor.matmul(
+                    level3[:, j, :],
+                    kept["product2", u][:, 1, j, :],
+                    diagonal3[:],
+                    start=False,
+                    stop=False,
+                )
+            for j in range(n):
+                add_turned(level3[:, j, :], product3[:, j, :], start=False, stop=(j == n - 1))
             channels = work.tile([P, n, P], F32, name=f"channels_{n}")
             nc.scalar.copy(channels[:], level3[:])
             first = UNITS[u][0]

import concourse.mybir as mybir
from concourse.masks import make_identity

F32 = mybir.dt.float32
U16 = mybir.dt.uint16
ALU = mybir.AluOpType
ACT = mybir.ActivationFunctionType
AXIS = mybir.AxisListType

P = 128
POSITIONS, ENTRIES = 512, 576
POSITION_BLOCKS = POSITIONS // P
UNITS = ((0, 1), (2,), (3,))
PSUM_BANKS = 8
TENSOR_RESTS = 2
LIST = 1024
LEVEL1 = LIST // 2
LEVEL1_BLOCKS = LEVEL1 // P
HALF1 = LEVEL1 // 2
PIECES = ((0, P), (P, HALF1), (HALF1, LEVEL1))
KINDS = 16
LOAD_ROWS = 64
GATE_BLOCKS = 7
LEVEL2_BLOCK, LEVEL3_BLOCK = 4, 6


def tile_logictreeconv2d_kernel(tc, x, logits, offs, out):
    nc = tc.nc
    with (
        tc.tile_pool(name="held", bufs=1) as held,
        tc.tile_pool(name="work", bufs=POSITION_BLOCKS) as work,
        tc.psum_pool(name="psum", bufs=PSUM_BANKS) as psum,
    ):
        rows = logits.rearrange("k (g n) -> (k g) n", n=P)
        first_rows = (0, KINDS * GATE_BLOCKS - LOAD_ROWS)
        kind_rows = [held.tile([LOAD_ROWS, P], F32, name=f"kind_rows{n}") for n in range(2)]
        for n, queue in enumerate((nc.sync, nc.scalar)):
            queue.dma_start(kind_rows[n][:], rows[first_rows[n] : first_rows[n] + LOAD_ROWS, :])

        offsets = held.tile([P, LIST // 16], U16, name="offsets")
        nc.sync.dma_start(offsets[:], offs)
        list_a = offsets[:, : LEVEL1 // 16]
        list_b = offsets[:, LEVEL1 // 16 :]

        windows = []
        for r in range(POSITION_BLOCKS):
            window = held.tile([P, ENTRIES], F32, name=f"window{r}")
            queue = nc.sync if r % 2 == 0 else nc.scalar
            queue.dma_start(window[:], x[r * P : (r + 1) * P, :])
            windows.append(window)

        identity = held.tile([P, P], F32, name="identity")
        make_identity(nc, identity[:])

        def add_turned(bank, block, start, stop):
            nc.tensor.matmul(
                bank, lhsT=block, rhs=identity[:], is_transpose=True, start=start, stop=stop
            )

        def spread(columns, name):
            row = held.tile([P, LEVEL1], F32, name=name)
            for lo, hi in PIECES:
                piece = psum.tile([P, hi - lo], F32, name="piece", tag="bank")
                for n in range(lo, hi, P):
                    nc.tensor.transpose(
                        piece[:, n - lo : n - lo + P],
                        columns[:, n // P : n // P + 1].to_broadcast([P, P]),
                        identity[:],
                    )
                nc.scalar.copy(row[:, lo:hi], piece[:])
            return row

        gate_kinds = psum.tile([P, KINDS * GATE_BLOCKS], F32, name="gate_kinds", tag="bank")
        for n in range(2):
            nc.tensor.transpose(
                gate_kinds[:, first_rows[n] : first_rows[n] + LOAD_ROWS],
                kind_rows[n][:],
                identity[:LOAD_ROWS, :LOAD_ROWS],
            )
        by_kind = gate_kinds[:].rearrange("p (k g) -> p k g", g=GATE_BLOCKS)

        minus_largest = held.tile([P, GATE_BLOCKS], F32, name="minus_largest")
        nc.vector.reduce_max(
            minus_largest[:], by_kind.rearrange("p k g -> p g k"), axis=AXIS.X, negate=True
        )
        exps = held.tile([P, GATE_BLOCKS, KINDS], F32, name="exps")
        sums = held.tile([P, GATE_BLOCKS], F32, name="sums")
        for g in range(GATE_BLOCKS):
            nc.scalar.activation(
                exps[:, g, :],
                by_kind[:, :, g],
                ACT.Exp,
                bias=minus_largest[:, g : g + 1],
                accum_out=sums[:, g : g + 1],
            )
        inverse_sum = held.tile([P, 1, GATE_BLOCKS], F32, name="inverse_sum")
        for lo, hi in (*PIECES, (LEVEL1, GATE_BLOCKS * P)):
            blocks = slice(lo // P, hi // P)
            nc.vector.reciprocal(inverse_sum[:, 0, blocks], sums[:, blocks])

        inverse_row = spread(inverse_sum[:, 0, :], "inverse_row")

        raw = held.tile([P, 4, GATE_BLOCKS], F32, name="raw")
        for place, bit in enumerate((3, 1, 2, 0)):
            with_bit = exps[:].rearrange("p g (hi two lo) -> p two g hi lo", two=2, lo=2**bit)
            nc.vector.reduce_sum(raw[:, place, :], with_bit[:, 1], axis=AXIS.XY)

        nc.vector.tensor_sub(raw[:, 3, :], raw[:, 3, :], raw[:, 1, :])
        nc.vector.tensor_sub(
            raw[:, 1:3, :], raw[:, 1:3, :], raw[:, 0:1, :].to_broadcast([P, 2, GATE_BLOCKS])
        )
        nc.vector.tensor_sub(raw[:, 3, :], raw[:, 3, :], raw[:, 2, :])
        weight = held.tile([P, 4, GATE_BLOCKS], F32, name="weight")
        nc.vector.tensor_mul(weight[:], raw[:], inverse_sum[:].to_broadcast([P, 4, GATE_BLOCKS]))

        raw2_row = spread(raw[:, 2, :], "raw2_row")

        diagonals = held.tile([P, LEVEL1_BLOCKS, P], F32, name="diagonals")
        for g in range(LEVEL1_BLOCKS):
            nc.scalar.activation(
                diagonals[:, g, :], identity[:], ACT.Copy, scale=raw[:, 2, g : g + 1]
            )
        diagonal3 = held.tile([P, P], F32, name="diagonal3")
        nc.scalar.activation(
            diagonal3[:], identity[:], ACT.Copy, scale=weight[:, 2, LEVEL3_BLOCK : LEVEL3_BLOCK + 1]
        )

        def affine(dest, b, bias, scale):
            nc.scalar.activation(dest, b, ACT.Identity, bias=bias, scale=scale)

        below_a = weight[:, 0, 0:2]
        below_b = weight[:, 0, 2:4]
        level2_w = [weight[:, t, LEVEL2_BLOCK : LEVEL2_BLOCK + 2] for t in range(4)]
        folded = held.tile([P, 3, 2], F32, name="folded")
        partly = held.tile([P, 2], F32, name="partly")
        for i in range(2):
            one = slice(i, i + 1)
            affine(folded[:, 1, one], below_b[:, one], bias=level2_w[1][:, one], scale=level2_w[3][:, one])
            affine(folded[:, 2, one], below_a[:, one], bias=level2_w[2][:, one], scale=level2_w[3][:, one])
            affine(partly[:, one], below_b[:, one], bias=level2_w[0][:, one], scale=level2_w[2][:, one])
            affine(folded[:, 0, one], below_a[:, one], bias=partly[:, one], scale=folded[:, 1, one])

        level3_w = [weight[:, t, LEVEL3_BLOCK : LEVEL3_BLOCK + 1] for t in range(4)]
        early = held.tile([P, 2, 2], F32, name="early")
        for which, (t_bias, t_scale) in enumerate(((1, 3), (0, 2))):
            affine(early[:, which, 0:1], folded[:, 0, 1:2], bias=level3_w[t_bias], scale=level3_w[t_scale])
            affine(early[:, which, 1:2], folded[:, 2, 1:2], bias=0.0, scale=level3_w[t_scale])

        kept = {}

        def pick_b(r):
            scaled_b = work.tile([P, LEVEL1], F32, name="scaled_b")
            for lo, hi in PIECES if r == 0 else ((0, LEVEL1),):
                nc.vector.tensor_tensor(
                    scaled_b[:, lo:hi],
                    windows[r][:].indirect(list_b[:, lo // 16 : hi // 16]),
                    inverse_row[:, lo:hi],
                    ALU.mult,
                )
            turned = psum.tile([P, LEVEL1_BLOCKS, P], F32, name="turned", tag="bank")
            for g in range(LEVEL1_BLOCKS):
                nc.tensor.transpose(turned[:, g, :], scaled_b[:, g * P : (g + 1) * P], identity[:])
            bracket_turned = work.tile([P, LEVEL1_BLOCKS, P], F32, name="bracket_turned")
            for g in range(LEVEL1_BLOCKS):
                affine(
                    bracket_turned[:, g, :],
                    turned[:, g, :],
                    bias=weight[:, 1, g : g + 1],
                    scale=raw[:, 3, g : g + 1],
                )
            kept["scaled_b", r], kept["turned", r] = scaled_b, turned
            kept["bracket_turned", r] = bracket_turned

        def turn_back(r):
            turned_back = psum.tile([P, LEVEL1], F32, name="turned_back", tag="bank")
            for g in range(LEVEL1_BLOCKS):
                nc.tensor.transpose(
                    turned_back[:, g * P : (g + 1) * P],
                    kept["bracket_turned", r][:, g, :],
                    identity[:],
                )
            bracket1 = work.tile([P, LEVEL1], F32, name="bracket1")
            nc.scalar.copy(bracket1[:], turned_back[:])
            kept["bracket1", r] = bracket1

        def rest_1(r):
            if r < TENSOR_RESTS:
                b_turned = work.tile([P, LEVEL1_BLOCKS, P], F32, name="b_turned")
                nc.scalar.copy(b_turned[:], kept["turned", r][:])
                kept["b_turned", r] = b_turned
            else:
                rest1 = work.tile([P, LEVEL1], F32, name="rest1")
                nc.vector.tensor_mul(rest1[:], kept["scaled_b", r][:], raw2_row[:])
                kept["rest1", r] = rest1

        def sum_rest(u, j):
            r, n = UNITS[u][j], len(UNITS[u])
            for h in (1, 0):
                if j == 0:
                    kept["level1", h, u] = psum.tile(
                        [P, HALF1 // P, n, P], F32, name="level1", tag="bank"
                    )
                for i in range(HALF1 // P):
                    g = h * (HALF1 // P) + i
                    part = kept["level1", h, u][:, i, j, :]
                    start = i == 0 and j == 0
                    if r < TENSOR_RESTS:
                        nc.tensor.matmul(
                            part,
                            diagonals[:, g, :],
                            kept["b_turned", r][:, g, :],
                            start=start,
                            stop=False,
                        )
                    else:
                        rest = kept["rest1", r][:, g * P : (g + 1) * P]
                        add_turned(part, rest, start=start, stop=False)

        def pick_a(u, j):
            r, n = UNITS[u][j], len(UNITS[u])
            product1 = work.tile([P, LEVEL1], F32, name="product1")
            nc.vector.tensor_tensor(
                product1[:], windows[r][:].indirect(list_a), kept["bracket1", r][:], ALU.mult
            )
            for h in (1, 0):
                for i in range(HALF1 // P):
                    g = h * (HALF1 // P) + i
                    add_turned(
                        kept["level1", h, u][:, i, j, :],
                        product1[:, g * P : (g + 1) * P],
                        start=False,
                        stop=(i == HALF1 // P - 1 and j == n - 1),
                    )

        def maps_2(u):
            n = len(UNITS[u])
            level1_b = kept["level1", 1, u]
            bracket2 = work.tile([P, 2, n, P], F32, name=f"bracket2_{n}")
            for i in range(2):
                affine(
                    bracket2[:, i, :, :],
                    level1_b[:, i, :, :],
                    bias=folded[:, 1, i : i + 1],
                    scale=level2_w[3][:, i : i + 1],
                )
            early3 = work.tile([P, 2, n, P], F32, name=f"early3_{n}")
            rest2 = work.tile([P, n, P], F32, name=f"rest2_{n}")
            affine(early3[:, 0, :, :], level1_b[:, 1, :, :], bias=early[:, 0, 0:1], scale=early[:, 0, 1:2])
            affine(rest2[:], level1_b[:, 0, :, :], bias=folded[:, 0, 0:1], scale=folded[:, 2, 0:1])
            affine(early3[:, 1, :, :], level1_b[:, 1, :, :], bias=early[:, 1, 0:1], scale=early[:, 1, 1:2])
            kept["bracket2", u], kept["early3", u], kept["rest2", u] = bracket2, early3, rest2

        def products_2(u):
            product2 = work.tile([P, 2, len(UNITS[u]), P], F32, name=f"product2_{len(UNITS[u])}")
            last = u == len(UNITS) - 1
            for blocks in (slice(1, 2), slice(0, 1)) if last else (slice(0, 2),):
                nc.vector.tensor_mul(
                    product2[:, blocks],
                    kept["level1", 0, u][:, blocks],
                    kept["bracket2", u][:, blocks],
                )
            kept["product2", u] = product2

        def factors_3(u):
            n = len(UNITS[u])
            product2 = kept["product2", u]
            bracket3 = work.tile([P, n, P], F32, name=f"bracket3_{n}")
            nc.vector.scalar_tensor_tensor(
                bracket3[:],
                product2[:, 1, :, :],
                level3_w[3],
                kept["early3", u][:, 0, :, :],
                op0=ALU.mult,
                op1=ALU.add,
            )
            level2_a = work.tile([P, n, P], F32, name=f"level2_a_{n}")
            nc.vector.tensor_add(level2_a[:], product2[:, 0, :, :], kept["rest2", u][:])
            kept["bracket3", u], kept["level2_a", u] = bracket3, level2_a

        def level_3(u):
            n = len(UNITS[u])
            product3 = work.tile([P, n, P], F32, name=f"product3_{n}")
            nc.vector.tensor_mul(product3[:], kept["level2_a", u][:], kept["bracket3", u][:])
            level3 = psum.tile([P, n, P], F32, name="level3", tag="bank")
            for j in range(n):
                early_rest = kept["early3", u][:, 1, j, :]
                add_turned(level3[:, j, :], early_rest, start=(j == 0), stop=False)
            for j in range(n):
                nc.tensor.matmul(
                    level3[:, j, :],
                    kept["product2", u][:, 1, j, :],
                    diagonal3[:],
                    start=False,
                    stop=False,
                )
            for j in range(n):
                add_turned(level3[:, j, :], product3[:, j, :], start=False, stop=(j == n - 1))
            channels = work.tile([P, n, P], F32, name=f"channels_{n}")
            nc.scalar.copy(channels[:], level3[:])
            first = UNITS[u][0]
            rows = out[first * P : (first + n) * P, :]
            nc.sync.dma_start(rows.rearrange("(j p) c -> p j c", p=P), channels[:])

        places = [(u, j) for u in range(len(UNITS)) for j in range(len(UNITS[u]))]
        for step in range(POSITION_BLOCKS + 3):
            if step < POSITION_BLOCKS:
                pick_b(step)
            if 1 <= step <= POSITION_BLOCKS:
                turn_back(step - 1)
                rest_1(step - 1)
            if 3 <= step:
                u, j = places[step - 3]
                sum_rest(u, j)
                pick_a(u, j)
                if j == len(UNITS[u]) - 1:
                    maps_2(u)
        for stage in (products_2, factors_3, level_3):
            for u in range(len(UNITS)):
                stage(u)
